import numpy as np
import ml_dtypes


def mxq(x, axis, fmt="e4m3"):
    dtype, down = {"e4m3": (ml_dtypes.float8_e4m3fn, 7), "e5m2": (ml_dtypes.float8_e5m2, 14)}[fmt]
    v = np.moveaxis(np.asarray(x, np.float32).astype(ml_dtypes.bfloat16).astype(np.float64), axis, -1)
    blocks = v.reshape(v.shape[:-1] + (-1, 32))
    amax = np.abs(blocks).max(-1, keepdims=True)
    byte = np.maximum(np.where(amax > 0, np.frexp(amax)[1] - 1 + 127, 0) - down, 1)
    scale = np.exp2(byte - 127.0)
    codes = (blocks / scale).astype(np.float32).astype(dtype).astype(np.float64)
    return np.moveaxis((codes * scale).reshape(v.shape), -1, axis)


WIDE = False


def mx_kscale(k):
    if not WIDE:
        return np.ones(k)
    levels = np.array([10, -10, 5, -5, 0])
    a = np.random.permutation(np.resize(levels, k // 512 * 4)).reshape(k // 512, 4)
    idx = np.arange(k)
    return np.exp2(a[idx // 512, idx % 128 // 32])


BF16 = ml_dtypes.bfloat16


def bf(x):
    return np.asarray(x, np.float32).astype(BF16)


def f64(x):
    return np.asarray(x).astype(np.float64)


B, N, DM, D, G, P = 12, 512, 1024, 512, 512, 128
W_LANG, W_GRAV = 0.7, 0.3
EPS = 1e-8


def setup_inputs():
    s = mx_kscale(D)
    return {"q": bf(np.random.standard_normal((B, N - P, D)) * 1.4 * s),
            "k": bf(np.random.standard_normal((B, N, D)) * 1.4 / s),
            "y": bf(np.random.standard_normal((B, N, D)) * 2.5),
            "v": bf(np.random.standard_normal((B, N, D)) * 2.0)}


def reference(q, k, y, v):
    y = f64(y)
    sq = np.sum(y * y, axis=-1)
    qq, kq = mxq(f64(q), 2, "e4m3"), mxq(f64(k), 2, "e4m3")
    yq, vq = mxq(y, 2, "e4m3"), mxq(f64(v), 1, "e4m3")
    res = []
    for hi in range(G, N + G, G):
        lo = max(hi - G, P)
        mask = np.arange(lo, hi)[:, None] >= np.arange(hi)[None, :]
        scores = (qq[:, lo - P:hi - P] @ kq[:, :hi].transpose(0, 2, 1)) / np.sqrt(D)
        scores = np.where(mask, scores, -np.inf)
        p = np.exp(scores - scores.max(-1, keepdims=True))
        a_lang = p / p.sum(-1, keepdims=True)
        gram = yq[:, lo:hi] @ yq[:, :hi].transpose(0, 2, 1)
        dist2 = np.maximum(sq[:, lo:hi, None] + sq[:, None, :hi] - 2.0 * gram, 0.0)
        kern = np.where(mask, np.exp(-dist2 / (2.0 * D)), 0.0)
        a_grav = kern / (kern.sum(-1, keepdims=True) + EPS)
        a = W_LANG * a_lang + W_GRAV * a_grav
        res.append(mxq(a, 2, "e4m3") @ vq[:, :hi])
    return np.concatenate(res, axis=1)

@@ -1,0 +1,337 @@
+import math
+from contextlib import ExitStack
+
+import concourse.mybir as mybir
+from concourse.masks import make_identity
+
+F32 = mybir.dt.float32
+BF16 = mybir.dt.bfloat16
+U32 = mybir.dt.uint32
+U8 = mybir.dt.uint8
+FP8X4 = mybir.dt.float8_e4m3fn_x4
+ALU = mybir.AluOpType
+ACT = mybir.ActivationFunctionType
+AXIS = mybir.AxisListType
+
+P = 128
+PACK = 4
+BATCH = 12
+POSITIONS = 512
+FEATURES = 512
+KEY_BLOCKS = POSITIONS // P
+QUERY_TILES = KEY_BLOCKS - 1
+W_LANG, W_GRAV = 0.7, 0.3
+EPS = 1e-8
+SCORE_SCALE = 1.0 / math.sqrt(FEATURES)
+MASKED = -1.0e30
+APART = 8
+MX_WIDTHS = (128, 256, 512)
+
+FLOPS = 3 * 2 * BATCH * QUERY_TILES * P * POSITIONS * FEATURES
+
+
+def tile_head_pa_t_kernel(tc, q, k, y, v, out):
+    nc = tc.nc
+    sources = {"q": q, "k": k, "y": y, "v": v}
+    row_tiles = {"q": QUERY_TILES, "k": KEY_BLOCKS, "y": KEY_BLOCKS, "v": KEY_BLOCKS}
+    mx_columns = {"q": QUERY_TILES * P, "k": POSITIONS, "y": POSITIONS, "v": FEATURES}
+
+    with ExitStack() as ctx:
+        const = ctx.enter_context(tc.tile_pool(name="const", bufs=1))
+        inputs = ctx.enter_context(tc.tile_pool(name="inputs", bufs=3))
+        group = ctx.enter_context(tc.tile_pool(name="group", bufs=2))
+        packed = ctx.enter_context(tc.tile_pool(name="packed", bufs=3))
+        norms = ctx.enter_context(tc.tile_pool(name="norms", bufs=3))
+        scratch = ctx.enter_context(tc.tile_pool(name="scratch", bufs=2))
+        work = ctx.enter_context(tc.tile_pool(name="work", bufs=3))
+        psum_turn = ctx.enter_context(tc.psum_pool(name="psum_turn", bufs=3))
+        psum_mm = ctx.enter_context(tc.psum_pool(name="psum_mm", bufs=5))
+
+        ident_f32 = const.tile([P, P], F32, name="ident_f32")
+        make_identity(nc, ident_f32[:])
+        ident_bf16 = const.tile([P, P], BF16, name="ident_bf16")
+        make_identity(nc, ident_bf16[:])
+        zero_block = const.tile([P, P], BF16, name="zero_block")
+        nc.gpsimd.memset(zero_block[:], 0.0)
+        mask = const.tile([P, P], F32, name="mask")
+        nc.gpsimd.memset(mask[:], 0.0)
+        nc.gpsimd.affine_select(
+            out=mask[:], in_=mask[:], compare_op=ALU.is_ge, fill=MASKED,
+            base=0, pattern=[[-1, P]], channel_multiplier=1,
+        )
+
+        raw = {}
+        turned = {}
+        grouped = {}
+        codes = {}
+        half_sq = {}
+        unread = {}
+        spread = {}
+        half_sq_rows = {}
+        unit = {}
+
+        def load(b):
+            for name in ("y", "k", "q", "v"):
+                rows = inputs.tile([P, row_tiles[name] * FEATURES], BF16, name=name + "_rows", tag=name + "_rows")
+                nc.sync.dma_start(
+                    out=rows[:].rearrange("p (r f) -> p r f", f=FEATURES),
+                    in_=sources[name][b].rearrange("(r p) f -> p r f", p=P),
+                )
+                raw[(name, b)] = rows
+
+        def squares(b, blocks):
+            if b not in half_sq:
+                half_sq[b] = norms.tile([P, KEY_BLOCKS], F32, name="half_sq")
+                unread[b] = scratch.tile([P, KEY_BLOCKS * FEATURES], BF16, name="unread")
+            for r in blocks:
+                cols = slice(r * FEATURES, (r + 1) * FEATURES)
+                nc.scalar.activation(
+                    out=unread[b][:, cols], in_=raw[("y", b)][:, cols], func=ACT.Square,
+                    scale=math.sqrt(0.5), accum_out=half_sq[b][:, r : r + 1],
+                )
+
+        def spread_half_sq(b):
+            bank = psum_mm.tile([P, POSITIONS], F32, name="spread", tag="mm")
+            for r in range(KEY_BLOCKS):
+                nc.tensor.matmul(
+                    bank[:, r * P : (r + 1) * P],
+                    lhsT=half_sq[b][:, r : r + 1].to_broadcast([P, P]),
+                    rhs=ident_f32[:], start=True, stop=True,
+                )
+            spread[b] = bank
+
+        def copy_half_sq_rows(b):
+            rows = norms.tile([P, POSITIONS], F32, name="half_sq_rows")
+            nc.scalar.copy(out=rows[:], in_=spread[b][:])
+            half_sq_rows[b] = rows
+
+        def turn_rows(name, b):
+            words = raw[(name, b)][:].bitcast(F32)
+            half = FEATURES // 2
+            banks = []
+            for r0 in range(0, row_tiles[name], 2):
+                n = min(2, row_tiles[name] - r0)
+                bank = psum_turn.tile([P, n, 2, P], F32, name="turned", tag="turn")
+                for r in range(n):
+                    for u in range(2):
+                        start = (r0 + r) * half + u * P
+                        nc.tensor.transpose(bank[:, r, u, :], words[:, start : start + P], ident_f32[:])
+                banks.append((r0, n, bank))
+            turned[(name, b)] = banks
+
+        def copy_turned_rows(name, b):
+            tile_ = group.tile([P, row_tiles[name] * P * PACK], BF16, name=name + "_grouped", tag=name + "_grouped", align_bytes=64)
+            words = tile_[:].bitcast(F32).rearrange("p (c u) -> p c u", u=2)
+            copy = nc.vector.tensor_copy if name == "q" else nc.scalar.copy
+            for r0, n, bank in turned[(name, b)]:
+                copy(
+                    out=words[:, r0 * P : (r0 + n) * P, :].rearrange("p (r c) u -> p r c u", r=n),
+                    in_=bank[:].rearrange("p r u c -> p r c u"),
+                )
+            grouped[(name, b)] = tile_
+
+        def regroup_values(b):
+            tile_ = group.tile([P, FEATURES * PACK], BF16, name="v_grouped", tag="v_grouped", align_bytes=64)
+            nc.vector.tensor_copy(
+                out=tile_[:].rearrange("p (c i t) -> p c t i", i=4, t=PACK),
+                in_=raw[("v", b)][:].rearrange("p (t c i) -> p c t i", i=4, t=PACK),
+            )
+            grouped[("v", b)] = tile_
+
+        def quantise(name, b):
+            columns = mx_columns[name]
+            words = packed.tile([P, columns], U32, name=name + "_words", tag=name + "_words", align_bytes=64)
+            scales = packed.tile([P, columns], U8, name=name + "_scales", tag=name + "_scales", align_bytes=64)
+            c0 = 0
+            while c0 < columns:
+                n = max(w for w in (128, 256, 512) if w <= columns - c0)
+                nc.vector.quantize_mx(
+                    out=words[:, c0 : c0 + n].bitcast(FP8X4),
+                    scales=scales[:, c0 : c0 + n],
+                    in_=grouped[(name, b)][:, c0 * PACK : (c0 + n) * PACK],
+                )
+                c0 += n
+            codes[(name, b)] = (words, scales)
+
+        def products(b, t):
+            width = (t + 2) * P
+            n = min(w for w in MX_WIDTHS if w >= width)
+            banks = {}
+            for kind, left, right, c0 in (("scores", "q", "k", t * P), ("gram", "y", "y", (t + 1) * P)):
+                bank = psum_mm.tile([P, POSITIONS], F32, name=kind, tag="mm")
+                nc.tensor.matmul_mx(
+                    out=bank[:, :n],
+                    lhsT=codes[(left, b)][0][:, c0 : c0 + P].bitcast(FP8X4),
+                    lhsT_scale=codes[(left, b)][1][:, c0 : c0 + P],
+                    rhs=codes[(right, b)][0][:, :n].bitcast(FP8X4),
+                    rhs_scale=codes[(right, b)][1][:, :n],
+                    start=True, stop=True,
+                )
+                banks[kind] = bank
+            unit[(b, t)] = banks
+
+        def softmax_shift(b, t):
+            tiles = unit[(b, t)]
+            width = (t + 2) * P
+            full = width - P
+            lang = work.tile([P, POSITIONS], F32, name="lang")
+            diag_min = work.tile([P, 1], F32, name="diag_min")
+            shift = work.tile([P, 1], F32, name="shift")
+            nc.vector.scalar_tensor_tensor(
+                out=lang[:, full:width], in0=tiles["scores"][:, full:width], scalar=-SCORE_SCALE,
+                in1=mask[:], op0=ALU.mult, op1=ALU.subtract,
+            )
+            nc.vector.tensor_reduce(out=diag_min[:], in_=lang[:, full:width], axis=AXIS.X, op=ALU.min)
+            nc.vector.tensor_scalar(
+                out=lang[:, :full], in0=tiles["scores"][:, :full], scalar1=-SCORE_SCALE,
+                scalar2=diag_min[:, 0:1], op0=ALU.mult, op1=ALU.min, accum_out=shift[:, 0:1],
+            )
+            tiles["lang"], tiles["shift"] = lang, shift
+
+        def kernel_exponent(b, t):
+            tiles = unit[(b, t)]
+            width = (t + 2) * P
+            full = width - P
+            own = half_sq[b][:, t + 1 : t + 2]
+            grav = work.tile([P, POSITIONS], F32, name="grav")
+            nc.vector.tensor_tensor(
+                out=grav[:, :width], in0=tiles["gram"][:, :width], in1=half_sq_rows[b][:, :width], op=ALU.subtract,
+            )
+            nc.vector.tensor_scalar(
+                out=grav[:, :full], in0=grav[:, :full], scalar1=own, scalar2=0.0, op0=ALU.subtract, op1=ALU.min,
+            )
+            nc.vector.scalar_tensor_tensor(
+                out=grav[:, full:width], in0=grav[:, full:width], scalar=own, in1=mask[:],
+                op0=ALU.subtract, op1=ALU.min,
+            )
+            tiles["grav"] = grav
+
+        def exponentials(b, t):
+            tiles = unit[(b, t)]
+            width = (t + 2) * P
+            sums = work.tile([P, 2, APART], F32, name="sums")
+            nc.scalar.activation(
+                out=tiles["lang"][:, :width], in_=tiles["lang"][:, :width], func=ACT.Exp,
+                scale=-1.0, bias=tiles["shift"][:, 0:1], accum_out=sums[:, 0, 0:1],
+            )
+            nc.scalar.activation(
+                out=tiles["grav"][:, :width], in_=tiles["grav"][:, :width], func=ACT.Exp,
+                scale=2.0 / (2.0 * FEATURES), accum_out=sums[:, 1, 0:1],
+            )
+            tiles["sums"] = sums
+
+        def blend(b, t):
+            tiles = unit[(b, t)]
+            width = (t + 2) * P
+            sums = tiles["sums"]
+            inverse = work.tile([P, 2], F32, name="inverse")
+            weights = work.tile([P, POSITIONS], BF16, name="weights")
+            nc.vector.tensor_scalar(
+                out=sums[:, 1, 0:1], in0=sums[:, 1, 0:1], scalar1=EPS, scalar2=1.0 / W_GRAV, op0=ALU.add, op1=ALU.mult,
+            )
+            nc.vector.reciprocal(out=inverse[:], in_=sums[:, :, 0])
+            nc.vector.tensor_scalar(
+                out=tiles["lang"][:, :width], in0=tiles["lang"][:, :width], scalar1=inverse[:, 0:1],
+                scalar2=W_LANG, op0=ALU.mult, op1=ALU.mult,
+            )
+            nc.vector.scalar_tensor_tensor(
+                out=weights[:, :width], in0=tiles["grav"][:, :width], scalar=inverse[:, 1:2],
+                in1=tiles["lang"][:, :width], op0=ALU.mult, op1=ALU.add,
+            )
+            tiles["weights"] = weights
+
+        def turn_weights(b, t):
+            tiles = unit[(b, t)]
+            bank = psum_turn.tile([P, KEY_BLOCKS, P], BF16, name="weights_turned", tag="turn")
+            for j in range(KEY_BLOCKS):
+                block = tiles["weights"][:, j * P : (j + 1) * P] if j <= t + 1 else zero_block[:]
+                nc.tensor.transpose(bank[:, j, :], block, ident_bf16[:])
+            tiles["weights_turned"] = bank
+
+        def copy_turned_weights(b, t):
+            tiles = unit[(b, t)]
+            tile_ = work.tile([P, P * PACK], BF16, name="weights_grouped", align_bytes=64)
+            nc.scalar.copy(
+                out=tile_[:].rearrange("p (i j) -> p i j", j=PACK),
+                in_=tiles["weights_turned"][:].rearrange("p j i -> p i j"),
+            )
+            tiles["weights_grouped"] = tile_
+
+        def quantise_weights(b, t):
+            tiles = unit[(b, t)]
+            words = work.tile([P, P], U32, name="weights_words", align_bytes=64)
+            scales = work.tile([P, P], U8, name="weights_scales", align_bytes=64)
+            nc.vector.quantize_mx(out=words[:].bitcast(FP8X4), scales=scales[:], in_=tiles["weights_grouped"][:])
+            tiles["weights_codes"] = (words, scales)
+
+        def value_product(b, t):
+            tiles = unit[(b, t)]
+            bank = psum_mm.tile([P, FEATURES], F32, name="result", tag="mm")
+            nc.tensor.matmul_mx(
+                out=bank[:],
+                lhsT=tiles["weights_codes"][0][:].bitcast(FP8X4), lhsT_scale=tiles["weights_codes"][1][:],
+                rhs=codes[("v", b)][0][:].bitcast(FP8X4), rhs_scale=codes[("v", b)][1][:],
+                start=True, stop=True,
+            )
+            tiles["result"] = bank
+
+        def store(b, t):
+            tiles = unit[(b, t)]
+            rows = work.tile([P, FEATURES], F32, name="result_rows")
+            nc.scalar.copy(out=rows[:], in_=tiles["result"][:])
+            nc.sync.dma_start(out=out[b, t * P : (t + 1) * P, :], in_=rows[:])
+
+        def in_range(b):
+            return 0 <= b < BATCH
+
+        turn_order = ("y", "k", "q")
+
+        for b in range(-3, BATCH + 1):
+            for t in range(QUERY_TILES):
+                now = b * QUERY_TILES + t
+                after = divmod(now + 1, QUERY_TILES)
+                one_back = divmod(now - 1, QUERY_TILES)
+                two_back = divmod(now - 2, QUERY_TILES)
+                last_turned = (turn_order[t - 1], b + 2 if t > 0 else b + 1)
+
+                if in_range(two_back[0]):
+                    copy_turned_weights(two_back[0], two_back[1])
+                if last_turned[0] != "q" and in_range(last_turned[1]):
+                    copy_turned_rows(last_turned[0], last_turned[1])
+                if t == 0 and in_range(b + 1):
+                    copy_half_sq_rows(b + 1)
+                if in_range(after[0]):
+                    products(after[0], after[1])
+                if in_range(b):
+                    softmax_shift(b, t)
+                if in_range(two_back[0]):
+                    quantise_weights(two_back[0], two_back[1])
+                    value_product(two_back[0], two_back[1])
+                if in_range(b):
+                    kernel_exponent(b, t)
+                    exponentials(b, t)
+                if in_range(one_back[0]):
+                    blend(one_back[0], one_back[1])
+                    turn_weights(one_back[0], one_back[1])
+                if t == 0:
+                    if in_range(b + 1):
+                        quantise("k", b + 1)
+                        copy_turned_rows("q", b + 1)
+                if t == 1:
+                    if in_range(b + 1):
+                        quantise("q", b + 1)
+                        regroup_values(b + 1)
+                if t == 2:
+                    if in_range(b + 2):
+                        quantise("y", b + 2)
+                    if in_range(b + 1):
+                        quantise("v", b + 1)
+                if in_range(two_back[0]):
+                    store(two_back[0], two_back[1])
+                if in_range(b + 2):
+                    turn_rows(turn_order[t], b + 2)
+                    squares(b + 2, range(t + 1 if t > 0 else 0, t + 2))
+                if t == 2 and in_range(b + 2):
+                    spread_half_sq(b + 2)
+                if t == 0 and in_range(b + 3):
+                    load(b + 3)

@@ -51,8 +51,10 @@ def tile_head_pa_t_kernel(tc, q, k, y, v, out):
         make_identity(nc, ident_f32[:])
         ident_bf16 = const.tile([P, P], BF16, name="ident_bf16")
         make_identity(nc, ident_bf16[:])
-        zero_block = const.tile([P, P], BF16, name="zero_block")
-        nc.gpsimd.memset(zero_block[:], 0.0)
+        weights_grouped = []
+        for t in range(QUERY_TILES):
+            weights_grouped.append(const.tile([P, P * PACK], BF16, name="weights_grouped%d" % t, align_bytes=64))
+            nc.vector.memset(weights_grouped[t][:], 0.0)
         mask = const.tile([P, P], F32, name="mask")
         nc.gpsimd.memset(mask[:], 0.0)
         nc.gpsimd.affine_select(
@@ -93,10 +95,8 @@ def tile_head_pa_t_kernel(tc, q, k, y, v, out):
         def spread_half_sq(b):
             bank = psum_mm.tile([P, POSITIONS], F32, name="spread", tag="mm")
             for r in range(KEY_BLOCKS):
-                nc.tensor.matmul(
-                    bank[:, r * P : (r + 1) * P],
-                    lhsT=half_sq[b][:, r : r + 1].to_broadcast([P, P]),
-                    rhs=ident_f32[:], start=True, stop=True,
+                nc.tensor.transpose(
+                    bank[:, r * P : (r + 1) * P], half_sq[b][:, r : r + 1].to_broadcast([P, P]), ident_f32[:]
                 )
             spread[b] = bank
 
@@ -155,18 +155,21 @@ def tile_head_pa_t_kernel(tc, q, k, y, v, out):
 
         def products(b, t):
             width = (t + 2) * P
-            n = min(w for w in MX_WIDTHS if w >= width)
             banks = {}
             for kind, left, right, c0 in (("scores", "q", "k", t * P), ("gram", "y", "y", (t + 1) * P)):
                 bank = psum_mm.tile([P, POSITIONS], F32, name=kind, tag="mm")
-                nc.tensor.matmul_mx(
-                    out=bank[:, :n],
-                    lhsT=codes[(left, b)][0][:, c0 : c0 + P].bitcast(FP8X4),
-                    lhsT_scale=codes[(left, b)][1][:, c0 : c0 + P],
-                    rhs=codes[(right, b)][0][:, :n].bitcast(FP8X4),
-                    rhs_scale=codes[(right, b)][1][:, :n],
-                    start=True, stop=True,
-                )
+                k0 = 0
+                while k0 < width:
+                    n = max(w for w in MX_WIDTHS if w <= width - k0)
+                    nc.tensor.matmul_mx(
+                        out=bank[:, k0 : k0 + n],
+                        lhsT=codes[(left, b)][0][:, c0 : c0 + P].bitcast(FP8X4),
+                        lhsT_scale=codes[(left, b)][1][:, c0 : c0 + P],
+                        rhs=codes[(right, b)][0][:, k0 : k0 + n].bitcast(FP8X4),
+                        rhs_scale=codes[(right, b)][1][:, k0 : k0 + n],
+                        start=True, stop=True,
+                    )
+                    k0 += n
                 banks[kind] = bank
             unit[(b, t)] = banks
 
@@ -242,26 +245,23 @@ def tile_head_pa_t_kernel(tc, q, k, y, v, out):
 
         def turn_weights(b, t):
             tiles = unit[(b, t)]
-            bank = psum_turn.tile([P, KEY_BLOCKS, P], BF16, name="weights_turned", tag="turn")
-            for j in range(KEY_BLOCKS):
-                block = tiles["weights"][:, j * P : (j + 1) * P] if j <= t + 1 else zero_block[:]
-                nc.tensor.transpose(bank[:, j, :], block, ident_bf16[:])
+            bank = psum_turn.tile([P, t + 2, P], BF16, name="weights_turned", tag="turn")
+            for j in range(t + 2):
+                nc.tensor.transpose(bank[:, j, :], tiles["weights"][:, j * P : (j + 1) * P], ident_bf16[:])
             tiles["weights_turned"] = bank
 
         def copy_turned_weights(b, t):
             tiles = unit[(b, t)]
-            tile_ = work.tile([P, P * PACK], BF16, name="weights_grouped", align_bytes=64)
             nc.scalar.copy(
-                out=tile_[:].rearrange("p (i j) -> p i j", j=PACK),
+                out=weights_grouped[t][:].rearrange("p (i j) -> p i j", j=PACK)[:, :, : t + 2],
                 in_=tiles["weights_turned"][:].rearrange("p j i -> p i j"),
             )
-            tiles["weights_grouped"] = tile_
 
         def quantise_weights(b, t):
             tiles = unit[(b, t)]
             words = work.tile([P, P], U32, name="weights_words", align_bytes=64)
             scales = work.tile([P, P], U8, name="weights_scales", align_bytes=64)
-            nc.vector.quantize_mx(out=words[:].bitcast(FP8X4), scales=scales[:], in_=tiles["weights_grouped"][:])
+            nc.vector.quantize_mx(out=words[:].bitcast(FP8X4), scales=scales[:], in_=weights_grouped[t][:])
             tiles["weights_codes"] = (words, scales)
 
         def value_product(b, t):

@@ -43,7 +43,7 @@ def tile_head_pa_t_kernel(tc, q, k, y, v, out):
         packed = ctx.enter_context(tc.tile_pool(name="packed", bufs=3))
         norms = ctx.enter_context(tc.tile_pool(name="norms", bufs=3))
         scratch = ctx.enter_context(tc.tile_pool(name="scratch", bufs=2))
-        work = ctx.enter_context(tc.tile_pool(name="work", bufs=3))
+        work = ctx.enter_context(tc.tile_pool(name="work", bufs=4))
         psum_turn = ctx.enter_context(tc.psum_pool(name="psum_turn", bufs=3))
         psum_mm = ctx.enter_context(tc.psum_pool(name="psum_mm", bufs=5))
 
@@ -173,41 +173,51 @@ def tile_head_pa_t_kernel(tc, q, k, y, v, out):
                 banks[kind] = bank
             unit[(b, t)] = banks
 
-        def softmax_shift(b, t):
-            tiles = unit[(b, t)]
-            width = (t + 2) * P
-            full = width - P
-            lang = work.tile([P, POSITIONS], F32, name="lang")
-            diag_min = work.tile([P, 1], F32, name="diag_min")
-            shift = work.tile([P, 1], F32, name="shift")
-            nc.vector.scalar_tensor_tensor(
-                out=lang[:, full:width], in0=tiles["scores"][:, full:width], scalar=-SCORE_SCALE,
-                in1=mask[:], op0=ALU.mult, op1=ALU.subtract,
-            )
-            nc.vector.tensor_reduce(out=diag_min[:], in_=lang[:, full:width], axis=AXIS.X, op=ALU.min)
-            nc.vector.tensor_scalar(
-                out=lang[:, :full], in0=tiles["scores"][:, :full], scalar1=-SCORE_SCALE,
-                scalar2=diag_min[:, 0:1], op0=ALU.mult, op1=ALU.min, accum_out=shift[:, 0:1],
-            )
-            tiles["lang"], tiles["shift"] = lang, shift
+        def width_of(t):
+            return (t + 2) * P
 
-        def kernel_exponent(b, t):
-            tiles = unit[(b, t)]
-            width = (t + 2) * P
-            full = width - P
-            own = half_sq[b][:, t + 1 : t + 2]
-            grav = work.tile([P, POSITIONS], F32, name="grav")
-            nc.vector.tensor_tensor(
-                out=grav[:, :width], in0=tiles["gram"][:, :width], in1=half_sq_rows[b][:, :width], op=ALU.subtract,
-            )
-            nc.vector.tensor_scalar(
-                out=grav[:, :full], in0=grav[:, :full], scalar1=own, scalar2=0.0, op0=ALU.subtract, op1=ALU.min,
-            )
+        def lang_diagonal(b, t):
+            tiles, width = unit[(b, t)], width_of(t)
+            tiles["lang"] = work.tile([P, POSITIONS], F32, name="lang")
             nc.vector.scalar_tensor_tensor(
-                out=grav[:, full:width], in0=grav[:, full:width], scalar=own, in1=mask[:],
-                op0=ALU.subtract, op1=ALU.min,
+                out=tiles["lang"][:, width - P : width], in0=tiles["scores"][:, width - P : width],
+                scalar=-SCORE_SCALE, in1=mask[:], op0=ALU.mult, op1=ALU.subtract,
             )
-            tiles["grav"] = grav
+
+        def lang_diagonal_minimum(b, t):
+            tiles, width = unit[(b, t)], width_of(t)
+            tiles["diag_min"] = work.tile([P, 1], F32, name="diag_min")
+            nc.vector.tensor_reduce(
+                out=tiles["diag_min"][:], in_=tiles["lang"][:, width - P : width], axis=AXIS.X, op=ALU.min
+            )
+
+        def lang_before_diagonal(b, t):
+            tiles, width = unit[(b, t)], width_of(t)
+            tiles["shift"] = work.tile([P, 1], F32, name="shift")
+            nc.vector.tensor_scalar(
+                out=tiles["lang"][:, : width - P], in0=tiles["scores"][:, : width - P], scalar1=-SCORE_SCALE,
+                scalar2=tiles["diag_min"][:, 0:1], op0=ALU.mult, op1=ALU.min, accum_out=tiles["shift"][:, 0:1],
+            )
+
+        def grav_minus_key_norms(b, t):
+            tiles, width = unit[(b, t)], width_of(t)
+            tiles["grav"] = work.tile([P, POSITIONS], F32, name="grav")
+            nc.vector.tensor_tensor(
+                out=tiles["grav"][:, :width], in0=tiles["gram"][:, :width], in1=half_sq_rows[b][:, :width],
+                op=ALU.subtract,
+            )
+
+        def grav_before_diagonal(b, t):
+            part = unit[(b, t)]["grav"][:, : width_of(t) - P]
+            nc.vector.tensor_scalar(
+                out=part, in0=part, scalar1=half_sq[b][:, t + 1 : t + 2], scalar2=0.0, op0=ALU.subtract, op1=ALU.min,
+            )
+
+        def grav_diagonal(b, t):
+            part = unit[(b, t)]["grav"][:, width_of(t) - P : width_of(t)]
+            nc.vector.scalar_tensor_tensor(
+                out=part, in0=part, scalar=half_sq[b][:, t + 1 : t + 2], in1=mask[:], op0=ALU.subtract, op1=ALU.min,
+            )
 
         def exponentials(b, t):
             tiles = unit[(b, t)]
@@ -223,25 +233,31 @@ def tile_head_pa_t_kernel(tc, q, k, y, v, out):
             )
             tiles["sums"] = sums
 
-        def blend(b, t):
-            tiles = unit[(b, t)]
-            width = (t + 2) * P
-            sums = tiles["sums"]
-            inverse = work.tile([P, 2], F32, name="inverse")
-            weights = work.tile([P, POSITIONS], BF16, name="weights")
+        def grav_denominator(b, t):
+            sums = unit[(b, t)]["sums"]
             nc.vector.tensor_scalar(
                 out=sums[:, 1, 0:1], in0=sums[:, 1, 0:1], scalar1=EPS, scalar2=1.0 / W_GRAV, op0=ALU.add, op1=ALU.mult,
             )
-            nc.vector.reciprocal(out=inverse[:], in_=sums[:, :, 0])
+
+        def inverses(b, t):
+            tiles = unit[(b, t)]
+            tiles["inverse"] = work.tile([P, 2], F32, name="inverse")
+            nc.vector.reciprocal(out=tiles["inverse"][:], in_=tiles["sums"][:, :, 0])
+
+        def lang_weights(b, t):
+            tiles, width = unit[(b, t)], width_of(t)
             nc.vector.tensor_scalar(
-                out=tiles["lang"][:, :width], in0=tiles["lang"][:, :width], scalar1=inverse[:, 0:1],
+                out=tiles["lang"][:, :width], in0=tiles["lang"][:, :width], scalar1=tiles["inverse"][:, 0:1],
                 scalar2=W_LANG, op0=ALU.mult, op1=ALU.mult,
             )
+
+        def blend(b, t):
+            tiles, width = unit[(b, t)], width_of(t)
+            tiles["weights"] = work.tile([P, POSITIONS], BF16, name="weights")
             nc.vector.scalar_tensor_tensor(
-                out=weights[:, :width], in0=tiles["grav"][:, :width], scalar=inverse[:, 1:2],
+                out=tiles["weights"][:, :width], in0=tiles["grav"][:, :width], scalar=tiles["inverse"][:, 1:2],
                 in1=tiles["lang"][:, :width], op0=ALU.mult, op1=ALU.add,
             )
-            tiles["weights"] = weights
 
         def turn_weights(b, t):
             tiles = unit[(b, t)]
@@ -285,49 +301,62 @@ def tile_head_pa_t_kernel(tc, q, k, y, v, out):
             return 0 <= b < BATCH
 
         turn_order = ("y", "k", "q")
+        ctx.enter_context(tc.manual_schedule())
 
-        for b in range(-3, BATCH + 1):
+        for b in range(-3, BATCH + 2):
             for t in range(QUERY_TILES):
                 now = b * QUERY_TILES + t
                 after = divmod(now + 1, QUERY_TILES)
-                one_back = divmod(now - 1, QUERY_TILES)
-                two_back = divmod(now - 2, QUERY_TILES)
+                back1 = divmod(now - 1, QUERY_TILES)
+                back2 = divmod(now - 2, QUERY_TILES)
+                back3 = divmod(now - 3, QUERY_TILES)
+                back4 = divmod(now - 4, QUERY_TILES)
                 last_turned = (turn_order[t - 1], b + 2 if t > 0 else b + 1)
+                attend, mix, finish = in_range(b), in_range(back2[0]), in_range(back3[0])
 
-                if in_range(two_back[0]):
-                    copy_turned_weights(two_back[0], two_back[1])
-                if last_turned[0] != "q" and in_range(last_turned[1]):
-                    copy_turned_rows(last_turned[0], last_turned[1])
-                if t == 0 and in_range(b + 1):
-                    copy_half_sq_rows(b + 1)
+                if in_range(back1[0]):
+                    exponentials(*back1)
+                if finish:
+                    copy_turned_weights(*back3)
                 if in_range(after[0]):
-                    products(after[0], after[1])
-                if in_range(b):
-                    softmax_shift(b, t)
-                if in_range(two_back[0]):
-                    quantise_weights(two_back[0], two_back[1])
-                    value_product(two_back[0], two_back[1])
-                if in_range(b):
-                    kernel_exponent(b, t)
-                    exponentials(b, t)
-                if in_range(one_back[0]):
-                    blend(one_back[0], one_back[1])
-                    turn_weights(one_back[0], one_back[1])
-                if t == 0:
-                    if in_range(b + 1):
-                        quantise("k", b + 1)
-                        copy_turned_rows("q", b + 1)
-                if t == 1:
-                    if in_range(b + 1):
-                        quantise("q", b + 1)
-                        regroup_values(b + 1)
-                if t == 2:
-                    if in_range(b + 2):
-                        quantise("y", b + 2)
-                    if in_range(b + 1):
-                        quantise("v", b + 1)
-                if in_range(two_back[0]):
-                    store(two_back[0], two_back[1])
+                    products(*after)
+                if attend:
+                    lang_diagonal(b, t)
+                    grav_minus_key_norms(b, t)
+                if mix:
+                    grav_denominator(*back2)
+                if attend:
+                    lang_diagonal_minimum(b, t)
+                    grav_before_diagonal(b, t)
+                if mix:
+                    inverses(*back2)
+                if attend:
+                    lang_before_diagonal(b, t)
+                    grav_diagonal(b, t)
+                if mix:
+                    lang_weights(*back2)
+                if last_turned[0] != "q" and in_range(last_turned[1]):
+                    copy_turned_rows(*last_turned)
+                if finish:
+                    quantise_weights(*back3)
+                    value_product(*back3)
+                if mix:
+                    blend(*back2)
+                    turn_weights(*back2)
+                if t == 0 and in_range(b + 1):
+                    quantise("k", b + 1)
+                    copy_turned_rows("q", b + 1)
+                if t == 1 and in_range(b + 1):
+                    quantise("q", b + 1)
+                    regroup_values(b + 1)
+                if t == 2 and in_range(b + 2):
+                    quantise("y", b + 2)
+                if t == 2 and in_range(b + 1):
+                    quantise("v", b + 1)
+                if t == 1 and in_range(b + 1):
+                    copy_half_sq_rows(b + 1)
+                if in_range(back4[0]):
+                    store(*back4)
                 if in_range(b + 2):
                     turn_rows(turn_order[t], b + 2)
                     squares(b + 2, range(t + 1 if t > 0 else 0, t + 2))

@@ -312,53 +312,56 @@ def tile_head_pa_t_kernel(tc, q, k, y, v, out):
                 back3 = divmod(now - 3, QUERY_TILES)
                 back4 = divmod(now - 4, QUERY_TILES)
                 last_turned = (turn_order[t - 1], b + 2 if t > 0 else b + 1)
-                attend, mix, finish = in_range(b), in_range(back2[0]), in_range(back3[0])
+                attend, mix = in_range(b), in_range(back2[0])
 
                 if in_range(back1[0]):
                     exponentials(*back1)
-                if finish:
-                    copy_turned_weights(*back3)
-                if in_range(after[0]):
-                    products(*after)
                 if attend:
                     lang_diagonal(b, t)
                     grav_minus_key_norms(b, t)
-                if mix:
-                    grav_denominator(*back2)
+                if in_range(back4[0]):
+                    quantise_weights(*back4)
+                    value_product(*back4)
+                if in_range(after[0]):
+                    products(*after)
                 if attend:
                     lang_diagonal_minimum(b, t)
                     grav_before_diagonal(b, t)
                 if mix:
-                    inverses(*back2)
+                    grav_denominator(*back2)
                 if attend:
                     lang_before_diagonal(b, t)
                     grav_diagonal(b, t)
                 if mix:
-                    lang_weights(*back2)
+                    inverses(*back2)
                 if last_turned[0] != "q" and in_range(last_turned[1]):
                     copy_turned_rows(*last_turned)
-                if finish:
-                    quantise_weights(*back3)
-                    value_product(*back3)
+                if in_range(b + 2):
+                    turn_rows(turn_order[t], b + 2)
+                if t == 0 and in_range(b + 1):
+                    quantise("k", b + 1)
+                if t == 1 and in_range(b + 1):
+                    quantise("q", b + 1)
+                if t == 2 and in_range(b + 2):
+                    quantise("y", b + 2)
+                if mix:
+                    lang_weights(*back2)
+                if t == 0 and in_range(b + 1):
+                    copy_turned_rows("q", b + 1)
+                if t == 1 and in_range(b + 1):
+                    regroup_values(b + 1)
+                if t == 2 and in_range(b + 1):
+                    quantise("v", b + 1)
                 if mix:
                     blend(*back2)
                     turn_weights(*back2)
-                if t == 0 and in_range(b + 1):
-                    quantise("k", b + 1)
-                    copy_turned_rows("q", b + 1)
-                if t == 1 and in_range(b + 1):
-                    quantise("q", b + 1)
-                    regroup_values(b + 1)
-                if t == 2 and in_range(b + 2):
-                    quantise("y", b + 2)
-                if t == 2 and in_range(b + 1):
-                    quantise("v", b + 1)
+                if in_range(back3[0]):
+                    copy_turned_weights(*back3)
                 if t == 1 and in_range(b + 1):
                     copy_half_sq_rows(b + 1)
                 if in_range(back4[0]):
                     store(*back4)
                 if in_range(b + 2):
-                    turn_rows(turn_order[t], b + 2)
                     squares(b + 2, range(t + 1 if t > 0 else 0, t + 2))
                 if t == 2 and in_range(b + 2):
                     spread_half_sq(b + 2)

@@ -319,21 +319,24 @@ def tile_head_pa_t_kernel(tc, q, k, y, v, out):
                 if attend:
                     lang_diagonal(b, t)
                     grav_minus_key_norms(b, t)
+                if mix:
+                    grav_denominator(*back2)
+                if attend:
+                    lang_diagonal_minimum(b, t)
                 if in_range(back4[0]):
                     quantise_weights(*back4)
                     value_product(*back4)
                 if in_range(after[0]):
                     products(*after)
-                if attend:
-                    lang_diagonal_minimum(b, t)
-                    grav_before_diagonal(b, t)
-                if mix:
-                    grav_denominator(*back2)
-                if attend:
-                    lang_before_diagonal(b, t)
-                    grav_diagonal(b, t)
                 if mix:
                     inverses(*back2)
+                if attend:
+                    grav_before_diagonal(b, t)
+                    lang_before_diagonal(b, t)
+                if mix:
+                    lang_weights(*back2)
+                if attend:
+                    grav_diagonal(b, t)
                 if last_turned[0] != "q" and in_range(last_turned[1]):
                     copy_turned_rows(*last_turned)
                 if in_range(b + 2):
@@ -345,24 +348,22 @@ def tile_head_pa_t_kernel(tc, q, k, y, v, out):
                 if t == 2 and in_range(b + 2):
                     quantise("y", b + 2)
                 if mix:
-                    lang_weights(*back2)
+                    blend(*back2)
+                    turn_weights(*back2)
                 if t == 0 and in_range(b + 1):
                     copy_turned_rows("q", b + 1)
                 if t == 1 and in_range(b + 1):
                     regroup_values(b + 1)
                 if t == 2 and in_range(b + 1):
                     quantise("v", b + 1)
-                if mix:
-                    blend(*back2)
-                    turn_weights(*back2)
                 if in_range(back3[0]):
                     copy_turned_weights(*back3)
                 if t == 1 and in_range(b + 1):
                     copy_half_sq_rows(b + 1)
-                if in_range(back4[0]):
-                    store(*back4)
                 if in_range(b + 2):
                     squares(b + 2, range(t + 1 if t > 0 else 0, t + 2))
+                if in_range(back4[0]):
+                    store(*back4)
                 if t == 2 and in_range(b + 2):
                     spread_half_sq(b + 2)
                 if t == 0 and in_range(b + 3):

@@ -24,10 +24,22 @@ W_LANG, W_GRAV = 0.7, 0.3
 EPS = 1e-8
 SCORE_SCALE = 1.0 / math.sqrt(FEATURES)
 MASKED = -1.0e30
-APART = 8
-MX_WIDTHS = (128, 256, 512)
+BLOCK_F32 = 8
+POWERS = (128, 256, 512)
+LOADS_AHEAD = 3
+ROUNDS_TO_DRAIN = 4
 
 FLOPS = 3 * 2 * BATCH * QUERY_TILES * P * POSITIONS * FEATURES
+
+
+def power_pieces(columns):
+    pieces = []
+    start = 0
+    while start < columns:
+        size = max(w for w in POWERS if w <= columns - start)
+        pieces.append((start, size))
+        start += size
+    return pieces
 
 
 def tile_head_pa_t_kernel(tc, q, k, y, v, out):
@@ -38,14 +50,14 @@ def tile_head_pa_t_kernel(tc, q, k, y, v, out):
 
     with ExitStack() as ctx:
         const = ctx.enter_context(tc.tile_pool(name="const", bufs=1))
-        inputs = ctx.enter_context(tc.tile_pool(name="inputs", bufs=3))
+        inputs = ctx.enter_context(tc.tile_pool(name="inputs", bufs=LOADS_AHEAD))
         group = ctx.enter_context(tc.tile_pool(name="group", bufs=2))
         packed = ctx.enter_context(tc.tile_pool(name="packed", bufs=3))
         norms = ctx.enter_context(tc.tile_pool(name="norms", bufs=3))
         scratch = ctx.enter_context(tc.tile_pool(name="scratch", bufs=2))
         work = ctx.enter_context(tc.tile_pool(name="work", bufs=4))
-        psum_turn = ctx.enter_context(tc.psum_pool(name="psum_turn", bufs=3))
-        psum_mm = ctx.enter_context(tc.psum_pool(name="psum_mm", bufs=5))
+        psum_transposed = ctx.enter_context(tc.psum_pool(name="psum_transposed", bufs=3))
+        psum_products = ctx.enter_context(tc.psum_pool(name="psum_products", bufs=5))
 
         ident_f32 = const.tile([P, P], F32, name="ident_f32")
         make_identity(nc, ident_f32[:])
@@ -62,105 +74,119 @@ def tile_head_pa_t_kernel(tc, q, k, y, v, out):
             base=0, pattern=[[-1, P]], channel_multiplier=1,
         )
 
-        raw = {}
-        turned = {}
+        rows = {}
+        transposed = {}
         grouped = {}
         codes = {}
         half_sq = {}
-        unread = {}
-        spread = {}
-        half_sq_rows = {}
-        unit = {}
+        squares_unread = {}
+        half_sq_spread = {}
+        half_sq_of_keys = {}
+        state = {}
+
+        def in_batch(b):
+            return 0 <= b < BATCH
+
+        def width_of(t):
+            return (t + 2) * P
+
 
         def load(b):
+            if not in_batch(b):
+                return
             for name in ("y", "k", "q", "v"):
-                rows = inputs.tile([P, row_tiles[name] * FEATURES], BF16, name=name + "_rows", tag=name + "_rows")
+                rows[(name, b)] = inputs.tile([P, row_tiles[name] * FEATURES], BF16, name=name + "_rows")
                 nc.sync.dma_start(
-                    out=rows[:].rearrange("p (r f) -> p r f", f=FEATURES),
+                    out=rows[(name, b)][:].rearrange("p (r f) -> p r f", f=FEATURES),
                     in_=sources[name][b].rearrange("(r p) f -> p r f", p=P),
                 )
-                raw[(name, b)] = rows
 
-        def squares(b, blocks):
+        def sum_squares(b, key_blocks):
+            if not in_batch(b):
+                return
             if b not in half_sq:
                 half_sq[b] = norms.tile([P, KEY_BLOCKS], F32, name="half_sq")
-                unread[b] = scratch.tile([P, KEY_BLOCKS * FEATURES], BF16, name="unread")
-            for r in blocks:
+                squares_unread[b] = scratch.tile([P, KEY_BLOCKS * FEATURES], BF16, name="squares_unread")
+            for r in key_blocks:
                 cols = slice(r * FEATURES, (r + 1) * FEATURES)
                 nc.scalar.activation(
-                    out=unread[b][:, cols], in_=raw[("y", b)][:, cols], func=ACT.Square,
+                    out=squares_unread[b][:, cols], in_=rows[("y", b)][:, cols], func=ACT.Square,
                     scale=math.sqrt(0.5), accum_out=half_sq[b][:, r : r + 1],
                 )
 
         def spread_half_sq(b):
-            bank = psum_mm.tile([P, POSITIONS], F32, name="spread", tag="mm")
+            if not in_batch(b):
+                return
+            half_sq_spread[b] = psum_products.tile([P, POSITIONS], F32, name="half_sq_spread", tag="products")
             for r in range(KEY_BLOCKS):
                 nc.tensor.transpose(
-                    bank[:, r * P : (r + 1) * P], half_sq[b][:, r : r + 1].to_broadcast([P, P]), ident_f32[:]
+                    half_sq_spread[b][:, r * P : (r + 1) * P],
+                    half_sq[b][:, r : r + 1].to_broadcast([P, P]),
+                    ident_f32[:],
                 )
-            spread[b] = bank
 
-        def copy_half_sq_rows(b):
-            rows = norms.tile([P, POSITIONS], F32, name="half_sq_rows")
-            nc.scalar.copy(out=rows[:], in_=spread[b][:])
-            half_sq_rows[b] = rows
+        def copy_half_sq_spread(b):
+            if not in_batch(b):
+                return
+            half_sq_of_keys[b] = norms.tile([P, POSITIONS], F32, name="half_sq_of_keys")
+            nc.scalar.copy(out=half_sq_of_keys[b][:], in_=half_sq_spread[b][:])
 
-        def turn_rows(name, b):
-            words = raw[(name, b)][:].bitcast(F32)
-            half = FEATURES // 2
-            banks = []
+        def transpose_rows(name, b):
+            if not in_batch(b):
+                return
+            words = rows[(name, b)][:].bitcast(F32)
+            words_in_row = FEATURES // 2
+            transposed[(name, b)] = []
             for r0 in range(0, row_tiles[name], 2):
                 n = min(2, row_tiles[name] - r0)
-                bank = psum_turn.tile([P, n, 2, P], F32, name="turned", tag="turn")
+                bank = psum_transposed.tile([P, n, 2, P], F32, name="rows_transposed", tag="transposed")
                 for r in range(n):
                     for u in range(2):
-                        start = (r0 + r) * half + u * P
-                        nc.tensor.transpose(bank[:, r, u, :], words[:, start : start + P], ident_f32[:])
-                banks.append((r0, n, bank))
-            turned[(name, b)] = banks
+                        first = (r0 + r) * words_in_row + u * P
+                        nc.tensor.transpose(bank[:, r, u, :], words[:, first : first + P], ident_f32[:])
+                transposed[(name, b)].append((r0, n, bank))
 
-        def copy_turned_rows(name, b):
-            tile_ = group.tile([P, row_tiles[name] * P * PACK], BF16, name=name + "_grouped", tag=name + "_grouped", align_bytes=64)
-            words = tile_[:].bitcast(F32).rearrange("p (c u) -> p c u", u=2)
-            copy = nc.vector.tensor_copy if name == "q" else nc.scalar.copy
-            for r0, n, bank in turned[(name, b)]:
+        def copy_transposed_rows(name, b, copy):
+            if not in_batch(b):
+                return
+            grouped[(name, b)] = group.tile([P, mx_columns[name] * PACK], BF16, name=name + "_grouped", align_bytes=64)
+            words = grouped[(name, b)][:].bitcast(F32).rearrange("p (c u) -> p c u", u=2)
+            for r0, n, bank in transposed[(name, b)]:
                 copy(
                     out=words[:, r0 * P : (r0 + n) * P, :].rearrange("p (r c) u -> p r c u", r=n),
                     in_=bank[:].rearrange("p r u c -> p r c u"),
                 )
-            grouped[(name, b)] = tile_
 
         def regroup_values(b):
-            tile_ = group.tile([P, FEATURES * PACK], BF16, name="v_grouped", tag="v_grouped", align_bytes=64)
+            if not in_batch(b):
+                return
+            grouped[("v", b)] = group.tile([P, FEATURES * PACK], BF16, name="v_grouped", align_bytes=64)
             nc.vector.tensor_copy(
-                out=tile_[:].rearrange("p (c i t) -> p c t i", i=4, t=PACK),
-                in_=raw[("v", b)][:].rearrange("p (t c i) -> p c t i", i=4, t=PACK),
+                out=grouped[("v", b)][:].rearrange("p (f i c) -> p f c i", i=4, c=PACK),
+                in_=rows[("v", b)][:].rearrange("p (c f i) -> p f c i", i=4, c=PACK),
             )
-            grouped[("v", b)] = tile_
 
         def quantise(name, b):
-            columns = mx_columns[name]
-            words = packed.tile([P, columns], U32, name=name + "_words", tag=name + "_words", align_bytes=64)
-            scales = packed.tile([P, columns], U8, name=name + "_scales", tag=name + "_scales", align_bytes=64)
-            c0 = 0
-            while c0 < columns:
-                n = max(w for w in (128, 256, 512) if w <= columns - c0)
+            if not in_batch(b):
+                return
+            words = packed.tile([P, mx_columns[name]], U32, name=name + "_words", align_bytes=64)
+            scales = packed.tile([P, mx_columns[name]], U8, name=name + "_scales", align_bytes=64)
+            for c0, n in power_pieces(mx_columns[name]):
                 nc.vector.quantize_mx(
                     out=words[:, c0 : c0 + n].bitcast(FP8X4),
                     scales=scales[:, c0 : c0 + n],
                     in_=grouped[(name, b)][:, c0 * PACK : (c0 + n) * PACK],
                 )
-                c0 += n
             codes[(name, b)] = (words, scales)
 
+
         def products(b, t):
-            width = (t + 2) * P
-            banks = {}
+            if not in_batch(b):
+                return
+            state[(b, t)] = {}
             for kind, left, right, c0 in (("scores", "q", "k", t * P), ("gram", "y", "y", (t + 1) * P)):
-                bank = psum_mm.tile([P, POSITIONS], F32, name=kind, tag="mm")
-                k0 = 0
-                while k0 < width:
-                    n = max(w for w in MX_WIDTHS if w <= width - k0)
+                bank = psum_products.tile([P, POSITIONS], F32, name=kind, tag="products")
+                for k0, n in power_pieces(width_of(t)):
                     nc.tensor.matmul_mx(
                         out=bank[:, k0 : k0 + n],
                         lhsT=codes[(left, b)][0][:, c0 : c0 + P].bitcast(FP8X4),
@@ -169,15 +195,12 @@ def tile_head_pa_t_kernel(tc, q, k, y, v, out):
                         rhs_scale=codes[(right, b)][1][:, k0 : k0 + n],
                         start=True, stop=True,
                     )
-                    k0 += n
-                banks[kind] = bank
-            unit[(b, t)] = banks
-
-        def width_of(t):
-            return (t + 2) * P
+                state[(b, t)][kind] = bank
 
         def lang_diagonal(b, t):
-            tiles, width = unit[(b, t)], width_of(t)
+            if not in_batch(b):
+                return
+            tiles, width = state[(b, t)], width_of(t)
             tiles["lang"] = work.tile([P, POSITIONS], F32, name="lang")
             nc.vector.scalar_tensor_tensor(
                 out=tiles["lang"][:, width - P : width], in0=tiles["scores"][:, width - P : width],
@@ -185,186 +208,193 @@ def tile_head_pa_t_kernel(tc, q, k, y, v, out):
             )
 
         def lang_diagonal_minimum(b, t):
-            tiles, width = unit[(b, t)], width_of(t)
-            tiles["diag_min"] = work.tile([P, 1], F32, name="diag_min")
+            if not in_batch(b):
+                return
+            tiles, width = state[(b, t)], width_of(t)
+            tiles["diagonal_minimum"] = work.tile([P, 1], F32, name="diagonal_minimum")
             nc.vector.tensor_reduce(
-                out=tiles["diag_min"][:], in_=tiles["lang"][:, width - P : width], axis=AXIS.X, op=ALU.min
+                out=tiles["diagonal_minimum"][:], in_=tiles["lang"][:, width - P : width], axis=AXIS.X, op=ALU.min
             )
 
         def lang_before_diagonal(b, t):
-            tiles, width = unit[(b, t)], width_of(t)
+            if not in_batch(b):
+                return
+            tiles, width = state[(b, t)], width_of(t)
             tiles["shift"] = work.tile([P, 1], F32, name="shift")
             nc.vector.tensor_scalar(
                 out=tiles["lang"][:, : width - P], in0=tiles["scores"][:, : width - P], scalar1=-SCORE_SCALE,
-                scalar2=tiles["diag_min"][:, 0:1], op0=ALU.mult, op1=ALU.min, accum_out=tiles["shift"][:, 0:1],
+                scalar2=tiles["diagonal_minimum"][:, 0:1], op0=ALU.mult, op1=ALU.min,
+                accum_out=tiles["shift"][:, 0:1],
             )
 
         def grav_minus_key_norms(b, t):
-            tiles, width = unit[(b, t)], width_of(t)
+            if not in_batch(b):
+                return
+            tiles, width = state[(b, t)], width_of(t)
             tiles["grav"] = work.tile([P, POSITIONS], F32, name="grav")
             nc.vector.tensor_tensor(
-                out=tiles["grav"][:, :width], in0=tiles["gram"][:, :width], in1=half_sq_rows[b][:, :width],
+                out=tiles["grav"][:, :width], in0=tiles["gram"][:, :width], in1=half_sq_of_keys[b][:, :width],
                 op=ALU.subtract,
             )
 
         def grav_before_diagonal(b, t):
-            part = unit[(b, t)]["grav"][:, : width_of(t) - P]
+            if not in_batch(b):
+                return
+            part = state[(b, t)]["grav"][:, : width_of(t) - P]
             nc.vector.tensor_scalar(
                 out=part, in0=part, scalar1=half_sq[b][:, t + 1 : t + 2], scalar2=0.0, op0=ALU.subtract, op1=ALU.min,
             )
 
         def grav_diagonal(b, t):
-            part = unit[(b, t)]["grav"][:, width_of(t) - P : width_of(t)]
+            if not in_batch(b):
+                return
+            part = state[(b, t)]["grav"][:, width_of(t) - P : width_of(t)]
             nc.vector.scalar_tensor_tensor(
                 out=part, in0=part, scalar=half_sq[b][:, t + 1 : t + 2], in1=mask[:], op0=ALU.subtract, op1=ALU.min,
             )
 
         def exponentials(b, t):
-            tiles = unit[(b, t)]
-            width = (t + 2) * P
-            sums = work.tile([P, 2, APART], F32, name="sums")
+            if not in_batch(b):
+                return
+            tiles, width = state[(b, t)], width_of(t)
+            tiles["sums"] = work.tile([P, 2, BLOCK_F32], F32, name="sums")
             nc.scalar.activation(
                 out=tiles["lang"][:, :width], in_=tiles["lang"][:, :width], func=ACT.Exp,
-                scale=-1.0, bias=tiles["shift"][:, 0:1], accum_out=sums[:, 0, 0:1],
+                scale=-1.0, bias=tiles["shift"][:, 0:1], accum_out=tiles["sums"][:, 0, 0:1],
             )
             nc.scalar.activation(
                 out=tiles["grav"][:, :width], in_=tiles["grav"][:, :width], func=ACT.Exp,
-                scale=2.0 / (2.0 * FEATURES), accum_out=sums[:, 1, 0:1],
+                scale=2.0 / (2.0 * FEATURES), accum_out=tiles["sums"][:, 1, 0:1],
             )
-            tiles["sums"] = sums
 
         def grav_denominator(b, t):
-            sums = unit[(b, t)]["sums"]
+            if not in_batch(b):
+                return
+            kern_sum = state[(b, t)]["sums"][:, 1, 0:1]
             nc.vector.tensor_scalar(
-                out=sums[:, 1, 0:1], in0=sums[:, 1, 0:1], scalar1=EPS, scalar2=1.0 / W_GRAV, op0=ALU.add, op1=ALU.mult,
+                out=kern_sum, in0=kern_sum, scalar1=EPS, scalar2=1.0 / W_GRAV, op0=ALU.add, op1=ALU.mult,
             )
 
         def inverses(b, t):
-            tiles = unit[(b, t)]
+            if not in_batch(b):
+                return
+            tiles = state[(b, t)]
             tiles["inverse"] = work.tile([P, 2], F32, name="inverse")
             nc.vector.reciprocal(out=tiles["inverse"][:], in_=tiles["sums"][:, :, 0])
 
         def lang_weights(b, t):
-            tiles, width = unit[(b, t)], width_of(t)
+            if not in_batch(b):
+                return
+            tiles, width = state[(b, t)], width_of(t)
             nc.vector.tensor_scalar(
                 out=tiles["lang"][:, :width], in0=tiles["lang"][:, :width], scalar1=tiles["inverse"][:, 0:1],
                 scalar2=W_LANG, op0=ALU.mult, op1=ALU.mult,
             )
 
         def blend(b, t):
-            tiles, width = unit[(b, t)], width_of(t)
+            if not in_batch(b):
+                return
+            tiles, width = state[(b, t)], width_of(t)
             tiles["weights"] = work.tile([P, POSITIONS], BF16, name="weights")
             nc.vector.scalar_tensor_tensor(
                 out=tiles["weights"][:, :width], in0=tiles["grav"][:, :width], scalar=tiles["inverse"][:, 1:2],
                 in1=tiles["lang"][:, :width], op0=ALU.mult, op1=ALU.add,
             )
 
-        def turn_weights(b, t):
-            tiles = unit[(b, t)]
-            bank = psum_turn.tile([P, t + 2, P], BF16, name="weights_turned", tag="turn")
-            for j in range(t + 2):
-                nc.tensor.transpose(bank[:, j, :], tiles["weights"][:, j * P : (j + 1) * P], ident_bf16[:])
-            tiles["weights_turned"] = bank
+        def transpose_weights(b, t):
+            if not in_batch(b):
+                return
+            tiles = state[(b, t)]
+            bank = psum_transposed.tile([P, t + 2, P], BF16, name="weights_transposed", tag="transposed")
+            for c in range(t + 2):
+                nc.tensor.transpose(bank[:, c, :], tiles["weights"][:, c * P : (c + 1) * P], ident_bf16[:])
+            tiles["weights_transposed"] = bank
 
-        def copy_turned_weights(b, t):
-            tiles = unit[(b, t)]
+        def copy_transposed_weights(b, t):
+            if not in_batch(b):
+                return
             nc.scalar.copy(
-                out=weights_grouped[t][:].rearrange("p (i j) -> p i j", j=PACK)[:, :, : t + 2],
-                in_=tiles["weights_turned"][:].rearrange("p j i -> p i j"),
+                out=weights_grouped[t][:].rearrange("p (i c) -> p i c", c=PACK)[:, :, : t + 2],
+                in_=state[(b, t)]["weights_transposed"][:].rearrange("p c i -> p i c"),
             )
 
         def quantise_weights(b, t):
-            tiles = unit[(b, t)]
+            if not in_batch(b):
+                return
             words = work.tile([P, P], U32, name="weights_words", align_bytes=64)
             scales = work.tile([P, P], U8, name="weights_scales", align_bytes=64)
             nc.vector.quantize_mx(out=words[:].bitcast(FP8X4), scales=scales[:], in_=weights_grouped[t][:])
-            tiles["weights_codes"] = (words, scales)
+            state[(b, t)]["weights_codes"] = (words, scales)
 
         def value_product(b, t):
-            tiles = unit[(b, t)]
-            bank = psum_mm.tile([P, FEATURES], F32, name="result", tag="mm")
+            if not in_batch(b):
+                return
+            tiles = state[(b, t)]
+            tiles["result"] = psum_products.tile([P, FEATURES], F32, name="result", tag="products")
             nc.tensor.matmul_mx(
-                out=bank[:],
+                out=tiles["result"][:],
                 lhsT=tiles["weights_codes"][0][:].bitcast(FP8X4), lhsT_scale=tiles["weights_codes"][1][:],
                 rhs=codes[("v", b)][0][:].bitcast(FP8X4), rhs_scale=codes[("v", b)][1][:],
                 start=True, stop=True,
             )
-            tiles["result"] = bank
 
         def store(b, t):
-            tiles = unit[(b, t)]
-            rows = work.tile([P, FEATURES], F32, name="result_rows")
-            nc.scalar.copy(out=rows[:], in_=tiles["result"][:])
-            nc.sync.dma_start(out=out[b, t * P : (t + 1) * P, :], in_=rows[:])
+            if not in_batch(b):
+                return
+            result_rows = work.tile([P, FEATURES], F32, name="result_rows")
+            nc.scalar.copy(out=result_rows[:], in_=state[(b, t)]["result"][:])
+            nc.sync.dma_start(out=out[b, t * P : (t + 1) * P, :], in_=result_rows[:])
 
-        def in_range(b):
-            return 0 <= b < BATCH
-
-        turn_order = ("y", "k", "q")
         ctx.enter_context(tc.manual_schedule())
 
-        for b in range(-3, BATCH + 2):
-            for t in range(QUERY_TILES):
-                now = b * QUERY_TILES + t
-                after = divmod(now + 1, QUERY_TILES)
-                back1 = divmod(now - 1, QUERY_TILES)
-                back2 = divmod(now - 2, QUERY_TILES)
-                back3 = divmod(now - 3, QUERY_TILES)
-                back4 = divmod(now - 4, QUERY_TILES)
-                last_turned = (turn_order[t - 1], b + 2 if t > 0 else b + 1)
-                attend, mix = in_range(b), in_range(back2[0])
+        for n in range(-LOADS_AHEAD * QUERY_TILES, BATCH * QUERY_TILES + ROUNDS_TO_DRAIN):
+            b, t = divmod(n, QUERY_TILES)
+            entered = {back: divmod(n - back, QUERY_TILES) for back in range(-1, ROUNDS_TO_DRAIN + 1)}
 
-                if in_range(back1[0]):
-                    exponentials(*back1)
-                if attend:
-                    lang_diagonal(b, t)
-                    grav_minus_key_norms(b, t)
-                if mix:
-                    grav_denominator(*back2)
-                if attend:
-                    lang_diagonal_minimum(b, t)
-                if in_range(back4[0]):
-                    quantise_weights(*back4)
-                    value_product(*back4)
-                if in_range(after[0]):
-                    products(*after)
-                if mix:
-                    inverses(*back2)
-                if attend:
-                    grav_before_diagonal(b, t)
-                    lang_before_diagonal(b, t)
-                if mix:
-                    lang_weights(*back2)
-                if attend:
-                    grav_diagonal(b, t)
-                if last_turned[0] != "q" and in_range(last_turned[1]):
-                    copy_turned_rows(*last_turned)
-                if in_range(b + 2):
-                    turn_rows(turn_order[t], b + 2)
-                if t == 0 and in_range(b + 1):
-                    quantise("k", b + 1)
-                if t == 1 and in_range(b + 1):
-                    quantise("q", b + 1)
-                if t == 2 and in_range(b + 2):
-                    quantise("y", b + 2)
-                if mix:
-                    blend(*back2)
-                    turn_weights(*back2)
-                if t == 0 and in_range(b + 1):
-                    copy_turned_rows("q", b + 1)
-                if t == 1 and in_range(b + 1):
-                    regroup_values(b + 1)
-                if t == 2 and in_range(b + 1):
-                    quantise("v", b + 1)
-                if in_range(back3[0]):
-                    copy_turned_weights(*back3)
-                if t == 1 and in_range(b + 1):
-                    copy_half_sq_rows(b + 1)
-                if in_range(b + 2):
-                    squares(b + 2, range(t + 1 if t > 0 else 0, t + 2))
-                if in_range(back4[0]):
-                    store(*back4)
-                if t == 2 and in_range(b + 2):
-                    spread_half_sq(b + 2)
-                if t == 0 and in_range(b + 3):
-                    load(b + 3)
+            exponentials(*entered[1])
+
+            grav_denominator(*entered[2])
+            lang_diagonal(b, t)
+            grav_minus_key_norms(b, t)
+            quantise_weights(*entered[4])
+
+            value_product(*entered[4])
+            products(*entered[-1])
+
+            inverses(*entered[2])
+            lang_diagonal_minimum(b, t)
+            grav_before_diagonal(b, t)
+            if t == 1:
+                copy_transposed_rows("y", b + 2, nc.scalar.copy)
+            if t == 2:
+                copy_transposed_rows("k", b + 2, nc.scalar.copy)
+            transpose_rows(("y", "k", "q")[t], b + 2)
+            if t == 0:
+                quantise("k", b + 1)
+            if t == 1:
+                quantise("q", b + 1)
+            if t == 2:
+                quantise("y", b + 2)
+
+            lang_weights(*entered[2])
+            lang_before_diagonal(b, t)
+            grav_diagonal(b, t)
+            if t == 0:
+                copy_transposed_rows("q", b + 1, nc.vector.tensor_copy)
+            if t == 1:
+                regroup_values(b + 1)
+            if t == 2:
+                quantise("v", b + 1)
+
+            blend(*entered[2])
+            transpose_weights(*entered[2])
+
+            copy_transposed_weights(*entered[3])
+            if t == 1:
+                copy_half_sq_spread(b + 1)
+            sum_squares(b + 2, range(t + 1 if t > 0 else 0, t + 2))
+            store(*entered[4])
+            if t == 2:
+                spread_half_sq(b + 2)
+            if t == 0:
+                load(b + LOADS_AHEAD)

@@ -26,6 +26,10 @@ SCORE_SCALE = 1.0 / math.sqrt(FEATURES)
 MASKED = -1.0e30
 BLOCK_F32 = 8
 POWERS = (128, 256, 512)
+PAIRS = FEATURES // 2
+PLANES = PAIRS // P
+TILES_IN_BANK = 2
+RUN = 4
 LOADS_AHEAD = 3
 ROUNDS_TO_DRAIN = 4
 
@@ -134,27 +138,26 @@ def tile_head_pa_t_kernel(tc, q, k, y, v, out):
         def transpose_rows(name, b):
             if not in_batch(b):
                 return
-            words = rows[(name, b)][:].bitcast(F32)
-            words_in_row = FEATURES // 2
+            pairs = rows[(name, b)][:].bitcast(F32)
             transposed[(name, b)] = []
-            for r0 in range(0, row_tiles[name], 2):
-                n = min(2, row_tiles[name] - r0)
-                bank = psum_transposed.tile([P, n, 2, P], F32, name="rows_transposed", tag="transposed")
-                for r in range(n):
-                    for u in range(2):
-                        first = (r0 + r) * words_in_row + u * P
-                        nc.tensor.transpose(bank[:, r, u, :], words[:, first : first + P], ident_f32[:])
-                transposed[(name, b)].append((r0, n, bank))
+            for r0 in range(0, row_tiles[name], TILES_IN_BANK):
+                count = min(TILES_IN_BANK, row_tiles[name] - r0)
+                bank = psum_transposed.tile([P, count, PLANES, P], F32, name="rows_transposed", tag="transposed")
+                for r in range(count):
+                    for u in range(PLANES):
+                        first = (r0 + r) * PAIRS + u * P
+                        nc.tensor.transpose(bank[:, r, u, :], pairs[:, first : first + P], ident_f32[:])
+                transposed[(name, b)].append((r0, count, bank))
 
         def copy_transposed_rows(name, b, copy):
             if not in_batch(b):
                 return
             grouped[(name, b)] = group.tile([P, mx_columns[name] * PACK], BF16, name=name + "_grouped", align_bytes=64)
-            words = grouped[(name, b)][:].bitcast(F32).rearrange("p (c u) -> p c u", u=2)
-            for r0, n, bank in transposed[(name, b)]:
+            pairs = grouped[(name, b)][:].bitcast(F32).rearrange("p (j u) -> p j u", u=PLANES)
+            for r0, count, bank in transposed[(name, b)]:
                 copy(
-                    out=words[:, r0 * P : (r0 + n) * P, :].rearrange("p (r c) u -> p r c u", r=n),
-                    in_=bank[:].rearrange("p r u c -> p r c u"),
+                    out=pairs[:, r0 * P : (r0 + count) * P, :].rearrange("p (r j) u -> p r j u", r=count),
+                    in_=bank[:].rearrange("p r u j -> p r j u"),
                 )
 
         def regroup_values(b):
@@ -162,8 +165,8 @@ def tile_head_pa_t_kernel(tc, q, k, y, v, out):
                 return
             grouped[("v", b)] = group.tile([P, FEATURES * PACK], BF16, name="v_grouped", align_bytes=64)
             nc.vector.tensor_copy(
-                out=grouped[("v", b)][:].rearrange("p (f i c) -> p f c i", i=4, c=PACK),
-                in_=rows[("v", b)][:].rearrange("p (c f i) -> p f c i", i=4, c=PACK),
+                out=grouped[("v", b)][:].rearrange("p (f i c) -> p f c i", i=RUN, c=PACK),
+                in_=rows[("v", b)][:].rearrange("p (c f i) -> p f c i", i=RUN, c=PACK),
             )
 
         def quantise(name, b):
@@ -171,11 +174,11 @@ def tile_head_pa_t_kernel(tc, q, k, y, v, out):
                 return
             words = packed.tile([P, mx_columns[name]], U32, name=name + "_words", align_bytes=64)
             scales = packed.tile([P, mx_columns[name]], U8, name=name + "_scales", align_bytes=64)
-            for c0, n in power_pieces(mx_columns[name]):
+            for c0, size in power_pieces(mx_columns[name]):
                 nc.vector.quantize_mx(
-                    out=words[:, c0 : c0 + n].bitcast(FP8X4),
-                    scales=scales[:, c0 : c0 + n],
-                    in_=grouped[(name, b)][:, c0 * PACK : (c0 + n) * PACK],
+                    out=words[:, c0 : c0 + size].bitcast(FP8X4),
+                    scales=scales[:, c0 : c0 + size],
+                    in_=grouped[(name, b)][:, c0 * PACK : (c0 + size) * PACK],
                 )
             codes[(name, b)] = (words, scales)
 
@@ -186,13 +189,13 @@ def tile_head_pa_t_kernel(tc, q, k, y, v, out):
             state[(b, t)] = {}
             for kind, left, right, c0 in (("scores", "q", "k", t * P), ("gram", "y", "y", (t + 1) * P)):
                 bank = psum_products.tile([P, POSITIONS], F32, name=kind, tag="products")
-                for k0, n in power_pieces(width_of(t)):
+                for k0, size in power_pieces(width_of(t)):
                     nc.tensor.matmul_mx(
-                        out=bank[:, k0 : k0 + n],
+                        out=bank[:, k0 : k0 + size],
                         lhsT=codes[(left, b)][0][:, c0 : c0 + P].bitcast(FP8X4),
                         lhsT_scale=codes[(left, b)][1][:, c0 : c0 + P],
-                        rhs=codes[(right, b)][0][:, k0 : k0 + n].bitcast(FP8X4),
-                        rhs_scale=codes[(right, b)][1][:, k0 : k0 + n],
+                        rhs=codes[(right, b)][0][:, k0 : k0 + size].bitcast(FP8X4),
+                        rhs_scale=codes[(right, b)][1][:, k0 : k0 + size],
                         start=True, stop=True,
                     )
                 state[(b, t)][kind] = bank
@@ -271,7 +274,7 @@ def tile_head_pa_t_kernel(tc, q, k, y, v, out):
             if not in_batch(b):
                 return
             kern_sum = state[(b, t)]["sums"][:, 1, 0:1]
-            nc.vector.tensor_scalar(
+            nc.gpsimd.tensor_scalar(
                 out=kern_sum, in0=kern_sum, scalar1=EPS, scalar2=1.0 / W_GRAV, op0=ALU.add, op1=ALU.mult,
             )
 
@@ -352,8 +355,8 @@ def tile_head_pa_t_kernel(tc, q, k, y, v, out):
             entered = {back: divmod(n - back, QUERY_TILES) for back in range(-1, ROUNDS_TO_DRAIN + 1)}
 
             exponentials(*entered[1])
+            grav_denominator(*entered[1])
 
-            grav_denominator(*entered[2])
             lang_diagonal(b, t)
             grav_minus_key_norms(b, t)
             quantise_weights(*entered[4])

@@ -29,9 +29,9 @@ POWERS = (128, 256, 512)
 PAIRS = FEATURES // 2
 PLANES = PAIRS // P
 TILES_IN_BANK = 2
-RUN = 4
+VALUE_PARTS = ((0, 128), (128, 128), (256, 256))
 LOADS_AHEAD = 3
-ROUNDS_TO_DRAIN = 4
+ROUNDS_TO_DRAIN = 5
 
 FLOPS = 3 * 2 * BATCH * QUERY_TILES * P * POSITIONS * FEATURES
 
@@ -57,6 +57,8 @@ def tile_head_pa_t_kernel(tc, q, k, y, v, out):
         inputs = ctx.enter_context(tc.tile_pool(name="inputs", bufs=LOADS_AHEAD))
         group = ctx.enter_context(tc.tile_pool(name="group", bufs=2))
         packed = ctx.enter_context(tc.tile_pool(name="packed", bufs=3))
+        value_group = ctx.enter_context(tc.tile_pool(name="value_group", bufs=1))
+        value_packed = ctx.enter_context(tc.tile_pool(name="value_packed", bufs=4))
         norms = ctx.enter_context(tc.tile_pool(name="norms", bufs=3))
         scratch = ctx.enter_context(tc.tile_pool(name="scratch", bufs=2))
         work = ctx.enter_context(tc.tile_pool(name="work", bufs=4))
@@ -83,6 +85,7 @@ def tile_head_pa_t_kernel(tc, q, k, y, v, out):
         grouped = {}
         codes = {}
         half_sq = {}
+        square = {}
         squares_unread = {}
         half_sq_spread = {}
         half_sq_of_keys = {}
@@ -105,17 +108,35 @@ def tile_head_pa_t_kernel(tc, q, k, y, v, out):
                     in_=sources[name][b].rearrange("(r p) f -> p r f", p=P),
                 )
 
-        def sum_squares(b, key_blocks):
+        def sum_squares(b):
             if not in_batch(b):
                 return
-            if b not in half_sq:
-                half_sq[b] = norms.tile([P, KEY_BLOCKS], F32, name="half_sq")
-                squares_unread[b] = scratch.tile([P, KEY_BLOCKS * FEATURES], BF16, name="squares_unread")
-            for r in key_blocks:
-                cols = slice(r * FEATURES, (r + 1) * FEATURES)
-                nc.scalar.activation(
-                    out=squares_unread[b][:, cols], in_=rows[("y", b)][:, cols], func=ACT.Square,
-                    scale=math.sqrt(0.5), accum_out=half_sq[b][:, r : r + 1],
+            half_sq[b] = norms.tile([P, KEY_BLOCKS], F32, name="half_sq")
+            squares_unread[b] = scratch.tile([P, FEATURES], BF16, name="squares_unread")
+            nc.scalar.activation(
+                out=squares_unread[b][:], in_=rows[("y", b)][:, :FEATURES], func=ACT.Square,
+                scale=math.sqrt(0.5), accum_out=half_sq[b][:, 0:1],
+            )
+
+        def square_products(b):
+            if not in_batch(b):
+                return
+            features = grouped[("y", b)][:].rearrange("p (j c) -> p c j", c=PACK)
+            bank = psum_products.tile([P, QUERY_TILES, P], F32, name="square", tag="products")
+            for t in range(QUERY_TILES):
+                for c in range(PACK):
+                    block = features[:, c, (t + 1) * P : (t + 2) * P]
+                    nc.tensor.matmul(bank[:, t, :], lhsT=block, rhs=block, start=c == 0, stop=c == PACK - 1)
+            square[b] = bank
+
+        def take_diagonals(b):
+            if not in_batch(b):
+                return
+            for t in range(QUERY_TILES):
+                diagonal_unread = scratch.tile([P, P], F32, name="diagonal_unread")
+                nc.vector.scalar_tensor_tensor(
+                    out=diagonal_unread[:], in0=square[b][:, t, :], scalar=0.5, in1=ident_f32[:],
+                    op0=ALU.mult, op1=ALU.mult, accum_out=half_sq[b][:, t + 1 : t + 2],
                 )
 
         def spread_half_sq(b):
@@ -160,13 +181,30 @@ def tile_head_pa_t_kernel(tc, q, k, y, v, out):
                     in_=bank[:].rearrange("p r u j -> p r j u"),
                 )
 
-        def regroup_values(b):
+        def regroup_values(b, part):
             if not in_batch(b):
                 return
-            grouped[("v", b)] = group.tile([P, FEATURES * PACK], BF16, name="v_grouped", align_bytes=64)
-            nc.vector.tensor_copy(
-                out=grouped[("v", b)][:].rearrange("p (f i c) -> p f c i", i=RUN, c=PACK),
-                in_=rows[("v", b)][:].rearrange("p (c f i) -> p f c i", i=RUN, c=PACK),
+            f0, size = VALUE_PARTS[part]
+            tile = value_group.tile([P, size * PACK], BF16, name="v_grouped%d" % part, align_bytes=64)
+            grouped[("v", b, part)] = tile
+            nc.gpsimd.tensor_scalar(
+                out=tile[:].rearrange("p (f c) -> p f c", c=PACK),
+                in0=rows[("v", b)][:].rearrange("p (c f) -> p f c", c=PACK)[:, f0 : f0 + size, :],
+                scalar1=1.0, scalar2=0.0, op0=ALU.mult, op1=ALU.add,
+            )
+
+        def quantise_values(b, part):
+            if not in_batch(b):
+                return
+            if part == 0:
+                words = value_packed.tile([P, FEATURES], U32, name="v_words", align_bytes=64)
+                scales = value_packed.tile([P, FEATURES], U8, name="v_scales", align_bytes=64)
+                codes[("v", b)] = (words, scales)
+            words, scales = codes[("v", b)]
+            f0, size = VALUE_PARTS[part]
+            nc.vector.quantize_mx(
+                out=words[:, f0 : f0 + size].bitcast(FP8X4), scales=scales[:, f0 : f0 + size],
+                in_=grouped[("v", b, part)][:],
             )
 
         def quantise(name, b):
@@ -223,11 +261,20 @@ def tile_head_pa_t_kernel(tc, q, k, y, v, out):
             if not in_batch(b):
                 return
             tiles, width = state[(b, t)], width_of(t)
-            tiles["shift"] = work.tile([P, 1], F32, name="shift")
+            tiles["before_minimum"] = work.tile([P, 1], F32, name="before_minimum")
             nc.vector.tensor_scalar(
                 out=tiles["lang"][:, : width - P], in0=tiles["scores"][:, : width - P], scalar1=-SCORE_SCALE,
-                scalar2=tiles["diagonal_minimum"][:, 0:1], op0=ALU.mult, op1=ALU.min,
-                accum_out=tiles["shift"][:, 0:1],
+                scalar2=None, op0=ALU.mult, op1=ALU.min, accum_out=tiles["before_minimum"][:, 0:1],
+            )
+
+        def row_minimum(b, t):
+            if not in_batch(b):
+                return
+            tiles = state[(b, t)]
+            tiles["shift"] = work.tile([P, 1], F32, name="shift")
+            nc.gpsimd.tensor_scalar(
+                out=tiles["shift"][:], in0=tiles["before_minimum"][:], scalar1=tiles["diagonal_minimum"][:, 0:1],
+                scalar2=None, op0=ALU.min,
             )
 
         def grav_minus_key_norms(b, t):
@@ -354,50 +401,53 @@ def tile_head_pa_t_kernel(tc, q, k, y, v, out):
             b, t = divmod(n, QUERY_TILES)
             entered = {back: divmod(n - back, QUERY_TILES) for back in range(-1, ROUNDS_TO_DRAIN + 1)}
 
+            store(*entered[5])
             exponentials(*entered[1])
             grav_denominator(*entered[1])
 
             lang_diagonal(b, t)
+            lang_before_diagonal(b, t)
             grav_minus_key_norms(b, t)
-            quantise_weights(*entered[4])
-
-            value_product(*entered[4])
-            products(*entered[-1])
-
-            inverses(*entered[2])
             lang_diagonal_minimum(b, t)
-            grav_before_diagonal(b, t)
+            row_minimum(b, t)
+            inverses(*entered[2])
+            if t == 0:
+                take_diagonals(b + 1)
+
+            if t == 0:
+                copy_transposed_rows("q", b + 1, nc.scalar.copy)
             if t == 1:
                 copy_transposed_rows("y", b + 2, nc.scalar.copy)
             if t == 2:
                 copy_transposed_rows("k", b + 2, nc.scalar.copy)
+
+            quantise_weights(*entered[4])
+            lang_weights(*entered[2])
+            grav_before_diagonal(b, t)
+
+            value_product(*entered[4])
+            products(*entered[-1])
+            if t == 2:
+                square_products(b + 2)
             transpose_rows(("y", "k", "q")[t], b + 2)
+
+            blend(*entered[2])
+            grav_diagonal(b, t)
             if t == 0:
                 quantise("k", b + 1)
             if t == 1:
                 quantise("q", b + 1)
             if t == 2:
                 quantise("y", b + 2)
-
-            lang_weights(*entered[2])
-            lang_before_diagonal(b, t)
-            grav_diagonal(b, t)
-            if t == 0:
-                copy_transposed_rows("q", b + 1, nc.vector.tensor_copy)
-            if t == 1:
-                regroup_values(b + 1)
-            if t == 2:
-                quantise("v", b + 1)
-
-            blend(*entered[2])
+            quantise_values(b + 1, t)
+            regroup_values(b + 2, t)
             transpose_weights(*entered[2])
 
             copy_transposed_weights(*entered[3])
             if t == 1:
                 copy_half_sq_spread(b + 1)
-            sum_squares(b + 2, range(t + 1 if t > 0 else 0, t + 2))
-            store(*entered[4])
-            if t == 2:
-                spread_half_sq(b + 2)
             if t == 0:
+                sum_squares(b + 2)
+            if t == 0:
+                spread_half_sq(b + 1)
                 load(b + LOADS_AHEAD)

@@ -227,15 +227,14 @@ def tile_head_pa_t_kernel(tc, q, k, y, v, out):
             state[(b, t)] = {}
             for kind, left, right, c0 in (("scores", "q", "k", t * P), ("gram", "y", "y", (t + 1) * P)):
                 bank = psum_products.tile([P, POSITIONS], F32, name=kind, tag="products")
-                for k0, size in power_pieces(width_of(t)):
-                    nc.tensor.matmul_mx(
-                        out=bank[:, k0 : k0 + size],
-                        lhsT=codes[(left, b)][0][:, c0 : c0 + P].bitcast(FP8X4),
-                        lhsT_scale=codes[(left, b)][1][:, c0 : c0 + P],
-                        rhs=codes[(right, b)][0][:, k0 : k0 + size].bitcast(FP8X4),
-                        rhs_scale=codes[(right, b)][1][:, k0 : k0 + size],
-                        start=True, stop=True,
-                    )
+                nc.tensor.matmul_mx(
+                    out=bank[:],
+                    lhsT=codes[(left, b)][0][:, c0 : c0 + P].bitcast(FP8X4),
+                    lhsT_scale=codes[(left, b)][1][:, c0 : c0 + P],
+                    rhs=codes[(right, b)][0][:].bitcast(FP8X4),
+                    rhs_scale=codes[(right, b)][1][:],
+                    start=True, stop=True,
+                )
                 state[(b, t)][kind] = bank
 
         def lang_diagonal(b, t):
@@ -405,12 +404,12 @@ def tile_head_pa_t_kernel(tc, q, k, y, v, out):
             exponentials(*entered[1])
             grav_denominator(*entered[1])
 
+            inverses(*entered[2])
             lang_diagonal(b, t)
             lang_before_diagonal(b, t)
             grav_minus_key_norms(b, t)
             lang_diagonal_minimum(b, t)
             row_minimum(b, t)
-            inverses(*entered[2])
             if t == 0:
                 take_diagonals(b + 1)
 
@@ -421,8 +420,8 @@ def tile_head_pa_t_kernel(tc, q, k, y, v, out):
             if t == 2:
                 copy_transposed_rows("k", b + 2, nc.scalar.copy)
 
-            quantise_weights(*entered[4])
             lang_weights(*entered[2])
+            quantise_weights(*entered[4])
             grav_before_diagonal(b, t)
 
             value_product(*entered[4])
@@ -431,14 +430,14 @@ def tile_head_pa_t_kernel(tc, q, k, y, v, out):
                 square_products(b + 2)
             transpose_rows(("y", "k", "q")[t], b + 2)
 
-            blend(*entered[2])
-            grav_diagonal(b, t)
             if t == 0:
                 quantise("k", b + 1)
             if t == 1:
                 quantise("q", b + 1)
             if t == 2:
                 quantise("y", b + 2)
+            blend(*entered[2])
+            grav_diagonal(b, t)
             quantise_values(b + 1, t)
             regroup_values(b + 2, t)
             transpose_weights(*entered[2])

@@ -227,15 +227,27 @@ def tile_head_pa_t_kernel(tc, q, k, y, v, out):
             state[(b, t)] = {}
             for kind, left, right, c0 in (("scores", "q", "k", t * P), ("gram", "y", "y", (t + 1) * P)):
                 bank = psum_products.tile([P, POSITIONS], F32, name=kind, tag="products")
+                for k0, size in power_pieces(width_of(t)):
+                    nc.tensor.matmul_mx(
+                        out=bank[:, k0 : k0 + size],
+                        lhsT=codes[(left, b)][0][:, c0 : c0 + P].bitcast(FP8X4),
+                        lhsT_scale=codes[(left, b)][1][:, c0 : c0 + P],
+                        rhs=codes[(right, b)][0][:, k0 : k0 + size].bitcast(FP8X4),
+                        rhs_scale=codes[(right, b)][1][:, k0 : k0 + size],
+                        start=True, stop=True,
+                    )
+                state[(b, t)][kind] = bank
+
+        def keep_warm(b, bank, columns, passes):
+            if not in_batch(b):
+                return
+            for i in range(passes):
                 nc.tensor.matmul_mx(
-                    out=bank[:],
-                    lhsT=codes[(left, b)][0][:, c0 : c0 + P].bitcast(FP8X4),
-                    lhsT_scale=codes[(left, b)][1][:, c0 : c0 + P],
-                    rhs=codes[(right, b)][0][:].bitcast(FP8X4),
-                    rhs_scale=codes[(right, b)][1][:],
+                    out=bank[:, POSITIONS - columns :],
+                    lhsT=codes[("k", b)][0][:, :P].bitcast(FP8X4), lhsT_scale=codes[("k", b)][1][:, :P],
+                    rhs=codes[("k", b)][0][:, :columns].bitcast(FP8X4), rhs_scale=codes[("k", b)][1][:, :columns],
                     start=True, stop=True,
                 )
-                state[(b, t)][kind] = bank
 
         def lang_diagonal(b, t):
             if not in_batch(b):
@@ -354,17 +366,19 @@ def tile_head_pa_t_kernel(tc, q, k, y, v, out):
             if not in_batch(b):
                 return
             tiles = state[(b, t)]
-            bank = psum_transposed.tile([P, t + 2, P], BF16, name="weights_transposed", tag="transposed")
+            bank = psum_transposed.tile([P, POSITIONS], F32, name="weights_transposed", tag="transposed")
+            keep_warm(b, bank, 2 * P, 4)
+            tiles["weights_transposed"] = bank[:, : 2 * P].bitcast(BF16)
             for c in range(t + 2):
-                nc.tensor.transpose(bank[:, c, :], tiles["weights"][:, c * P : (c + 1) * P], ident_bf16[:])
-            tiles["weights_transposed"] = bank
+                cols = slice(c * P, (c + 1) * P)
+                nc.tensor.transpose(tiles["weights_transposed"][:, cols], tiles["weights"][:, cols], ident_bf16[:])
 
         def copy_transposed_weights(b, t):
             if not in_batch(b):
                 return
             nc.scalar.copy(
                 out=weights_grouped[t][:].rearrange("p (i c) -> p i c", c=PACK)[:, :, : t + 2],
-                in_=state[(b, t)]["weights_transposed"][:].rearrange("p c i -> p i c"),
+                in_=state[(b, t)]["weights_transposed"][:, : (t + 2) * P].rearrange("p (c i) -> p i c", i=P),
             )
 
         def quantise_weights(b, t):
@@ -379,7 +393,6 @@ def tile_head_pa_t_kernel(tc, q, k, y, v, out):
             if not in_batch(b):
                 return
             tiles = state[(b, t)]
-            tiles["result"] = psum_products.tile([P, FEATURES], F32, name="result", tag="products")
             nc.tensor.matmul_mx(
                 out=tiles["result"][:],
                 lhsT=tiles["weights_codes"][0][:].bitcast(FP8X4), lhsT_scale=tiles["weights_codes"][1][:],
@@ -424,8 +437,11 @@ def tile_head_pa_t_kernel(tc, q, k, y, v, out):
             quantise_weights(*entered[4])
             grav_before_diagonal(b, t)
 
-            value_product(*entered[4])
             products(*entered[-1])
+            if in_batch(entered[4][0]):
+                state[entered[4]]["result"] = psum_products.tile([P, FEATURES], F32, name="result", tag="products")
+                keep_warm(b, state[entered[4]]["result"], POSITIONS, 2)
+            value_product(*entered[4])
             if t == 2:
                 square_products(b + 2)
             transpose_rows(("y", "k", "q")[t], b + 2)

@@ -238,17 +238,6 @@ def tile_head_pa_t_kernel(tc, q, k, y, v, out):
                     )
                 state[(b, t)][kind] = bank
 
-        def keep_warm(b, bank, columns, passes):
-            if not in_batch(b):
-                return
-            for i in range(passes):
-                nc.tensor.matmul_mx(
-                    out=bank[:, POSITIONS - columns :],
-                    lhsT=codes[("k", b)][0][:, :P].bitcast(FP8X4), lhsT_scale=codes[("k", b)][1][:, :P],
-                    rhs=codes[("k", b)][0][:, :columns].bitcast(FP8X4), rhs_scale=codes[("k", b)][1][:, :columns],
-                    start=True, stop=True,
-                )
-
         def lang_diagonal(b, t):
             if not in_batch(b):
                 return
@@ -366,19 +355,17 @@ def tile_head_pa_t_kernel(tc, q, k, y, v, out):
             if not in_batch(b):
                 return
             tiles = state[(b, t)]
-            bank = psum_transposed.tile([P, POSITIONS], F32, name="weights_transposed", tag="transposed")
-            keep_warm(b, bank, 2 * P, 4)
-            tiles["weights_transposed"] = bank[:, : 2 * P].bitcast(BF16)
+            bank = psum_transposed.tile([P, t + 2, P], BF16, name="weights_transposed", tag="transposed")
             for c in range(t + 2):
-                cols = slice(c * P, (c + 1) * P)
-                nc.tensor.transpose(tiles["weights_transposed"][:, cols], tiles["weights"][:, cols], ident_bf16[:])
+                nc.tensor.transpose(bank[:, c, :], tiles["weights"][:, c * P : (c + 1) * P], ident_bf16[:])
+            tiles["weights_transposed"] = bank
 
         def copy_transposed_weights(b, t):
             if not in_batch(b):
                 return
             nc.scalar.copy(
                 out=weights_grouped[t][:].rearrange("p (i c) -> p i c", c=PACK)[:, :, : t + 2],
-                in_=state[(b, t)]["weights_transposed"][:, : (t + 2) * P].rearrange("p (c i) -> p i c", i=P),
+                in_=state[(b, t)]["weights_transposed"][:].rearrange("p c i -> p i c"),
             )
 
         def quantise_weights(b, t):
@@ -393,6 +380,7 @@ def tile_head_pa_t_kernel(tc, q, k, y, v, out):
             if not in_batch(b):
                 return
             tiles = state[(b, t)]
+            tiles["result"] = psum_products.tile([P, FEATURES], F32, name="result", tag="products")
             nc.tensor.matmul_mx(
                 out=tiles["result"][:],
                 lhsT=tiles["weights_codes"][0][:].bitcast(FP8X4), lhsT_scale=tiles["weights_codes"][1][:],
@@ -438,9 +426,6 @@ def tile_head_pa_t_kernel(tc, q, k, y, v, out):
             grav_before_diagonal(b, t)
 
             products(*entered[-1])
-            if in_batch(entered[4][0]):
-                state[entered[4]]["result"] = psum_products.tile([P, FEATURES], F32, name="result", tag="products")
-                keep_warm(b, state[entered[4]]["result"], POSITIONS, 2)
             value_product(*entered[4])
             if t == 2:
                 square_products(b + 2)
@@ -454,8 +439,8 @@ def tile_head_pa_t_kernel(tc, q, k, y, v, out):
                 quantise("y", b + 2)
             blend(*entered[2])
             grav_diagonal(b, t)
-            quantise_values(b + 1, t)
-            regroup_values(b + 2, t)
+            quantise_values(b, t)
+            regroup_values(b + 1, t)
             transpose_weights(*entered[2])
 
             copy_transposed_weights(*entered[3])

@@ -29,7 +29,8 @@ POWERS = (128, 256, 512)
 PAIRS = FEATURES // 2
 PLANES = PAIRS // P
 TILES_IN_BANK = 2
-VALUE_PARTS = ((0, 128), (128, 128), (256, 256))
+VALUE_PARTS = ((0, 256), (256, 128), (384, 128))
+RUN = 4
 LOADS_AHEAD = 3
 ROUNDS_TO_DRAIN = 5
 
@@ -57,7 +58,7 @@ def tile_head_pa_t_kernel(tc, q, k, y, v, out):
         inputs = ctx.enter_context(tc.tile_pool(name="inputs", bufs=LOADS_AHEAD))
         group = ctx.enter_context(tc.tile_pool(name="group", bufs=2))
         packed = ctx.enter_context(tc.tile_pool(name="packed", bufs=3))
-        value_group = ctx.enter_context(tc.tile_pool(name="value_group", bufs=1))
+        value_group = ctx.enter_context(tc.tile_pool(name="value_group", bufs=2))
         value_packed = ctx.enter_context(tc.tile_pool(name="value_packed", bufs=4))
         norms = ctx.enter_context(tc.tile_pool(name="norms", bufs=3))
         scratch = ctx.enter_context(tc.tile_pool(name="scratch", bufs=2))
@@ -67,8 +68,6 @@ def tile_head_pa_t_kernel(tc, q, k, y, v, out):
 
         ident_f32 = const.tile([P, P], F32, name="ident_f32")
         make_identity(nc, ident_f32[:])
-        ident_bf16 = const.tile([P, P], BF16, name="ident_bf16")
-        make_identity(nc, ident_bf16[:])
         weights_grouped = []
         for t in range(QUERY_TILES):
             weights_grouped.append(const.tile([P, P * PACK], BF16, name="weights_grouped%d" % t, align_bytes=64))
@@ -187,10 +186,9 @@ def tile_head_pa_t_kernel(tc, q, k, y, v, out):
             f0, size = VALUE_PARTS[part]
             tile = value_group.tile([P, size * PACK], BF16, name="v_grouped%d" % part, align_bytes=64)
             grouped[("v", b, part)] = tile
-            nc.gpsimd.tensor_scalar(
-                out=tile[:].rearrange("p (f c) -> p f c", c=PACK),
-                in0=rows[("v", b)][:].rearrange("p (c f) -> p f c", c=PACK)[:, f0 : f0 + size, :],
-                scalar1=1.0, scalar2=0.0, op0=ALU.mult, op1=ALU.add,
+            nc.vector.tensor_copy(
+                out=tile[:].rearrange("p (f i c) -> p f c i", i=RUN, c=PACK),
+                in_=rows[("v", b)][:].rearrange("p (c f) -> p c f", c=PACK)[:, :, f0 : f0 + size].rearrange("p c (f i) -> p f c i", i=RUN),
             )
 
         def quantise_values(b, part):
@@ -261,10 +259,10 @@ def tile_head_pa_t_kernel(tc, q, k, y, v, out):
             if not in_batch(b):
                 return
             tiles, width = state[(b, t)], width_of(t)
-            tiles["before_minimum"] = work.tile([P, 1], F32, name="before_minimum")
+            tiles["shift"] = work.tile([P, 1], F32, name="shift")
             nc.vector.tensor_scalar(
                 out=tiles["lang"][:, : width - P], in0=tiles["scores"][:, : width - P], scalar1=-SCORE_SCALE,
-                scalar2=None, op0=ALU.mult, op1=ALU.min, accum_out=tiles["before_minimum"][:, 0:1],
+                scalar2=tiles["diagonal_minimum"][:, 0:1], op0=ALU.mult, op1=ALU.min, accum_out=tiles["shift"][:, 0:1],
             )
 
         def row_minimum(b, t):
@@ -341,23 +339,28 @@ def tile_head_pa_t_kernel(tc, q, k, y, v, out):
                 scalar2=W_LANG, op0=ALU.mult, op1=ALU.mult,
             )
 
-        def blend(b, t):
+        def grav_weights(b, t):
             if not in_batch(b):
                 return
             tiles, width = state[(b, t)], width_of(t)
-            tiles["weights"] = work.tile([P, POSITIONS], BF16, name="weights")
-            nc.vector.scalar_tensor_tensor(
-                out=tiles["weights"][:, :width], in0=tiles["grav"][:, :width], scalar=tiles["inverse"][:, 1:2],
-                in1=tiles["lang"][:, :width], op0=ALU.mult, op1=ALU.add,
+            nc.vector.tensor_scalar(
+                out=tiles["grav"][:, :width], in0=tiles["grav"][:, :width], scalar1=tiles["inverse"][:, 1:2],
+                scalar2=None, op0=ALU.mult,
             )
 
         def transpose_weights(b, t):
             if not in_batch(b):
                 return
             tiles = state[(b, t)]
-            bank = psum_transposed.tile([P, t + 2, P], BF16, name="weights_transposed", tag="transposed")
+            bank = psum_transposed.tile([P, t + 2, P], F32, name="weights_transposed", tag="transposed")
             for c in range(t + 2):
-                nc.tensor.transpose(bank[:, c, :], tiles["weights"][:, c * P : (c + 1) * P], ident_bf16[:])
+                cols = slice(c * P, (c + 1) * P)
+                nc.tensor.matmul(
+                    bank[:, c, :], lhsT=tiles["lang"][:, cols], rhs=ident_f32[:], is_transpose=True, start=True, stop=False
+                )
+                nc.tensor.matmul(
+                    bank[:, c, :], lhsT=tiles["grav"][:, cols], rhs=ident_f32[:], is_transpose=True, start=False, stop=True
+                )
             tiles["weights_transposed"] = bank
 
         def copy_transposed_weights(b, t):
@@ -405,12 +408,12 @@ def tile_head_pa_t_kernel(tc, q, k, y, v, out):
             exponentials(*entered[1])
             grav_denominator(*entered[1])
 
-            inverses(*entered[2])
             lang_diagonal(b, t)
-            lang_before_diagonal(b, t)
             grav_minus_key_norms(b, t)
+            inverses(*entered[2])
             lang_diagonal_minimum(b, t)
-            row_minimum(b, t)
+            regroup_values(b + 1, t)
+            lang_before_diagonal(b, t)
             if t == 0:
                 take_diagonals(b + 1)
 
@@ -437,10 +440,9 @@ def tile_head_pa_t_kernel(tc, q, k, y, v, out):
                 quantise("q", b + 1)
             if t == 2:
                 quantise("y", b + 2)
-            blend(*entered[2])
+            grav_weights(*entered[2])
             grav_diagonal(b, t)
             quantise_values(b, t)
-            regroup_values(b + 1, t)
             transpose_weights(*entered[2])
 
             copy_transposed_weights(*entered[3])

@@ -29,7 +29,7 @@ POWERS = (128, 256, 512)
 PAIRS = FEATURES // 2
 PLANES = PAIRS // P
 TILES_IN_BANK = 2
-VALUE_PARTS = ((0, 256), (256, 128), (384, 128))
+VALUE_PARTS = ((0, 128), (128, 128), (256, 128), (384, 128))
 RUN = 4
 LOADS_AHEAD = 3
 ROUNDS_TO_DRAIN = 5
@@ -58,7 +58,7 @@ def tile_head_pa_t_kernel(tc, q, k, y, v, out):
         inputs = ctx.enter_context(tc.tile_pool(name="inputs", bufs=LOADS_AHEAD))
         group = ctx.enter_context(tc.tile_pool(name="group", bufs=2))
         packed = ctx.enter_context(tc.tile_pool(name="packed", bufs=3))
-        value_group = ctx.enter_context(tc.tile_pool(name="value_group", bufs=2))
+        value_group = ctx.enter_context(tc.tile_pool(name="value_group", bufs=1))
         value_packed = ctx.enter_context(tc.tile_pool(name="value_packed", bufs=4))
         norms = ctx.enter_context(tc.tile_pool(name="norms", bufs=3))
         scratch = ctx.enter_context(tc.tile_pool(name="scratch", bufs=2))
@@ -186,10 +186,17 @@ def tile_head_pa_t_kernel(tc, q, k, y, v, out):
             f0, size = VALUE_PARTS[part]
             tile = value_group.tile([P, size * PACK], BF16, name="v_grouped%d" % part, align_bytes=64)
             grouped[("v", b, part)] = tile
-            nc.vector.tensor_copy(
-                out=tile[:].rearrange("p (f i c) -> p f c i", i=RUN, c=PACK),
-                in_=rows[("v", b)][:].rearrange("p (c f) -> p c f", c=PACK)[:, :, f0 : f0 + size].rearrange("p c (f i) -> p f c i", i=RUN),
-            )
+            if part == QUERY_TILES:
+                nc.vector.tensor_copy(
+                    out=tile[:].rearrange("p (f i c) -> p f c i", i=RUN, c=PACK),
+                    in_=rows[("v", b)][:].rearrange("p (c f) -> p c f", c=PACK)[:, :, f0 : f0 + size].rearrange("p c (f i) -> p f c i", i=RUN),
+                )
+            else:
+                nc.gpsimd.tensor_scalar(
+                    out=tile[:].rearrange("p (f c) -> p f c", c=PACK),
+                    in0=rows[("v", b)][:].rearrange("p (c f) -> p f c", c=PACK)[:, f0 : f0 + size, :],
+                    scalar1=1.0, scalar2=0.0, op0=ALU.mult, op1=ALU.add,
+                )
 
         def quantise_values(b, part):
             if not in_batch(b):
@@ -275,15 +282,17 @@ def tile_head_pa_t_kernel(tc, q, k, y, v, out):
                 scalar2=None, op0=ALU.min,
             )
 
-        def grav_minus_key_norms(b, t):
+        def grav_minus_key_norms(b, t, halves):
             if not in_batch(b):
                 return
             tiles, width = state[(b, t)], width_of(t)
-            tiles["grav"] = work.tile([P, POSITIONS], F32, name="grav")
-            nc.vector.tensor_tensor(
-                out=tiles["grav"][:, :width], in0=tiles["gram"][:, :width], in1=half_sq_of_keys[b][:, :width],
-                op=ALU.subtract,
-            )
+            if "grav" not in tiles:
+                tiles["grav"] = work.tile([P, POSITIONS], F32, name="grav")
+            for cols in (slice(0, width // 2), slice(width // 2, width))[halves]:
+                nc.vector.tensor_tensor(
+                    out=tiles["grav"][:, cols], in0=tiles["gram"][:, cols], in1=half_sq_of_keys[b][:, cols],
+                    op=ALU.subtract,
+                )
 
         def grav_before_diagonal(b, t):
             if not in_batch(b):
@@ -319,7 +328,7 @@ def tile_head_pa_t_kernel(tc, q, k, y, v, out):
             if not in_batch(b):
                 return
             kern_sum = state[(b, t)]["sums"][:, 1, 0:1]
-            nc.gpsimd.tensor_scalar(
+            nc.vector.tensor_scalar(
                 out=kern_sum, in0=kern_sum, scalar1=EPS, scalar2=1.0 / W_GRAV, op0=ALU.add, op1=ALU.mult,
             )
 
@@ -406,13 +415,13 @@ def tile_head_pa_t_kernel(tc, q, k, y, v, out):
 
             store(*entered[5])
             exponentials(*entered[1])
-            grav_denominator(*entered[1])
 
+            grav_denominator(*entered[2])
             lang_diagonal(b, t)
-            grav_minus_key_norms(b, t)
+            grav_minus_key_norms(b, t, slice(0, 1))
             inverses(*entered[2])
             lang_diagonal_minimum(b, t)
-            regroup_values(b + 1, t)
+            grav_minus_key_norms(b, t, slice(1, 2))
             lang_before_diagonal(b, t)
             if t == 0:
                 take_diagonals(b + 1)
@@ -442,7 +451,11 @@ def tile_head_pa_t_kernel(tc, q, k, y, v, out):
                 quantise("y", b + 2)
             grav_weights(*entered[2])
             grav_diagonal(b, t)
+            if t == 2:
+                quantise_values(b, 3)
+                regroup_values(b + 1, 3)
             quantise_values(b, t)
+            regroup_values(b + 1, t)
             transpose_weights(*entered[2])
 
             copy_transposed_weights(*entered[3])

@@ -29,8 +29,7 @@ POWERS = (128, 256, 512)
 PAIRS = FEATURES // 2
 PLANES = PAIRS // P
 TILES_IN_BANK = 2
-VALUE_PARTS = ((0, 128), (128, 128), (256, 128), (384, 128))
-RUN = 4
+VALUE_PARTS = ((0, 128), (128, 128), (256, 256))
 LOADS_AHEAD = 3
 ROUNDS_TO_DRAIN = 5
 
@@ -186,17 +185,11 @@ def tile_head_pa_t_kernel(tc, q, k, y, v, out):
             f0, size = VALUE_PARTS[part]
             tile = value_group.tile([P, size * PACK], BF16, name="v_grouped%d" % part, align_bytes=64)
             grouped[("v", b, part)] = tile
-            if part == QUERY_TILES:
-                nc.vector.tensor_copy(
-                    out=tile[:].rearrange("p (f i c) -> p f c i", i=RUN, c=PACK),
-                    in_=rows[("v", b)][:].rearrange("p (c f) -> p c f", c=PACK)[:, :, f0 : f0 + size].rearrange("p c (f i) -> p f c i", i=RUN),
-                )
-            else:
-                nc.gpsimd.tensor_scalar(
-                    out=tile[:].rearrange("p (f c) -> p f c", c=PACK),
-                    in0=rows[("v", b)][:].rearrange("p (c f) -> p f c", c=PACK)[:, f0 : f0 + size, :],
-                    scalar1=1.0, scalar2=0.0, op0=ALU.mult, op1=ALU.add,
-                )
+            nc.gpsimd.tensor_scalar(
+                out=tile[:].rearrange("p (f c) -> p f c", c=PACK),
+                in0=rows[("v", b)][:].rearrange("p (c f) -> p f c", c=PACK)[:, f0 : f0 + size, :],
+                scalar1=1.0, scalar2=0.0, op0=ALU.mult, op1=ALU.add,
+            )
 
         def quantise_values(b, part):
             if not in_batch(b):
@@ -407,22 +400,26 @@ def tile_head_pa_t_kernel(tc, q, k, y, v, out):
             nc.scalar.copy(out=result_rows[:], in_=state[(b, t)]["result"][:])
             nc.sync.dma_start(out=out[b, t * P : (t + 1) * P, :], in_=result_rows[:])
 
+        def tile_of(n):
+            b, r = divmod(n, QUERY_TILES)
+            return b, (r if b < BATCH - 1 else QUERY_TILES - 1 - r)
+
         ctx.enter_context(tc.manual_schedule())
 
         for n in range(-LOADS_AHEAD * QUERY_TILES, BATCH * QUERY_TILES + ROUNDS_TO_DRAIN):
             b, t = divmod(n, QUERY_TILES)
-            entered = {back: divmod(n - back, QUERY_TILES) for back in range(-1, ROUNDS_TO_DRAIN + 1)}
+            entered = {back: tile_of(n - back) for back in range(-1, ROUNDS_TO_DRAIN + 1)}
 
             store(*entered[5])
             exponentials(*entered[1])
 
+            lang_diagonal(*entered[0])
+            grav_minus_key_norms(*entered[0], slice(0, 1))
             grav_denominator(*entered[2])
-            lang_diagonal(b, t)
-            grav_minus_key_norms(b, t, slice(0, 1))
+            lang_diagonal_minimum(*entered[0])
+            grav_minus_key_norms(*entered[0], slice(1, 2))
             inverses(*entered[2])
-            lang_diagonal_minimum(b, t)
-            grav_minus_key_norms(b, t, slice(1, 2))
-            lang_before_diagonal(b, t)
+            lang_before_diagonal(*entered[0])
             if t == 0:
                 take_diagonals(b + 1)
 
@@ -435,7 +432,7 @@ def tile_head_pa_t_kernel(tc, q, k, y, v, out):
 
             lang_weights(*entered[2])
             quantise_weights(*entered[4])
-            grav_before_diagonal(b, t)
+            grav_before_diagonal(*entered[0])
 
             products(*entered[-1])
             value_product(*entered[4])
@@ -450,10 +447,7 @@ def tile_head_pa_t_kernel(tc, q, k, y, v, out):
             if t == 2:
                 quantise("y", b + 2)
             grav_weights(*entered[2])
-            grav_diagonal(b, t)
-            if t == 2:
-                quantise_values(b, 3)
-                regroup_values(b + 1, 3)
+            grav_diagonal(*entered[0])
             quantise_values(b, t)
             regroup_values(b + 1, t)
             transpose_weights(*entered[2])

import math
from contextlib import ExitStack

import concourse.mybir as mybir
from concourse.masks import make_identity

F32 = mybir.dt.float32
BF16 = mybir.dt.bfloat16
U32 = mybir.dt.uint32
U8 = mybir.dt.uint8
FP8X4 = mybir.dt.float8_e4m3fn_x4
ALU = mybir.AluOpType
ACT = mybir.ActivationFunctionType
AXIS = mybir.AxisListType

P = 128
PACK = 4
BATCH = 12
POSITIONS = 512
FEATURES = 512
KEY_BLOCKS = POSITIONS // P
QUERY_TILES = KEY_BLOCKS - 1
W_LANG, W_GRAV = 0.7, 0.3
EPS = 1e-8
SCORE_SCALE = 1.0 / math.sqrt(FEATURES)
MASKED = -1.0e30
BLOCK_F32 = 8
POWERS = (128, 256, 512)
PAIRS = FEATURES // 2
PLANES = PAIRS // P
TILES_IN_BANK = 2
VALUE_PARTS = ((0, 128), (128, 128), (256, 256))
LOADS_AHEAD = 3
ROUNDS_TO_DRAIN = 5

FLOPS = 3 * 2 * BATCH * QUERY_TILES * P * POSITIONS * FEATURES


def power_pieces(columns):
    pieces = []
    start = 0
    while start < columns:
        size = max(w for w in POWERS if w <= columns - start)
        pieces.append((start, size))
        start += size
    return pieces


def tile_head_pa_t_kernel(tc, q, k, y, v, out):
    nc = tc.nc
    sources = {"q": q, "k": k, "y": y, "v": v}
    row_tiles = {"q": QUERY_TILES, "k": KEY_BLOCKS, "y": KEY_BLOCKS, "v": KEY_BLOCKS}
    mx_columns = {"q": QUERY_TILES * P, "k": POSITIONS, "y": POSITIONS, "v": FEATURES}

    with ExitStack() as ctx:
        const = ctx.enter_context(tc.tile_pool(name="const", bufs=1))
        inputs = ctx.enter_context(tc.tile_pool(name="inputs", bufs=LOADS_AHEAD))
        group = ctx.enter_context(tc.tile_pool(name="group", bufs=2))
        packed = ctx.enter_context(tc.tile_pool(name="packed", bufs=3))
        value_group = ctx.enter_context(tc.tile_pool(name="value_group", bufs=1))
        value_packed = ctx.enter_context(tc.tile_pool(name="value_packed", bufs=4))
        norms = ctx.enter_context(tc.tile_pool(name="norms", bufs=3))
        scratch = ctx.enter_context(tc.tile_pool(name="scratch", bufs=2))
        work = ctx.enter_context(tc.tile_pool(name="work", bufs=4))
        psum_transposed = ctx.enter_context(tc.psum_pool(name="psum_transposed", bufs=3))
        psum_products = ctx.enter_context(tc.psum_pool(name="psum_products", bufs=5))

        ident_f32 = const.tile([P, P], F32, name="ident_f32")
        make_identity(nc, ident_f32[:])
        weights_grouped = []
        for t in range(QUERY_TILES):
            weights_grouped.append(const.tile([P, P * PACK], BF16, name="weights_grouped%d" % t, align_bytes=64))
            nc.vector.memset(weights_grouped[t][:], 0.0)
        mask = const.tile([P, P], F32, name="mask")
        nc.gpsimd.memset(mask[:], 0.0)
        nc.gpsimd.affine_select(
            out=mask[:], in_=mask[:], compare_op=ALU.is_ge, fill=MASKED,
            base=0, pattern=[[-1, P]], channel_multiplier=1,
        )

        rows = {}
        transposed = {}
        grouped = {}
        codes = {}
        half_sq = {}
        square = {}
        squares_unread = {}
        half_sq_spread = {}
        half_sq_of_keys = {}
        state = {}

        def in_batch(b):
            return 0 <= b < BATCH

        def width_of(t):
            return (t + 2) * P


        def load(b):
            if not in_batch(b):
                return
            for name in ("y", "k", "q", "v"):
                rows[(name, b)] = inputs.tile([P, row_tiles[name] * FEATURES], BF16, name=name + "_rows")
                nc.sync.dma_start(
                    out=rows[(name, b)][:].rearrange("p (r f) -> p r f", f=FEATURES),
                    in_=sources[name][b].rearrange("(r p) f -> p r f", p=P),
                )

        def sum_squares(b):
            if not in_batch(b):
                return
            half_sq[b] = norms.tile([P, KEY_BLOCKS], F32, name="half_sq")
            squares_unread[b] = scratch.tile([P, FEATURES], BF16, name="squares_unread")
            nc.scalar.activation(
                out=squares_unread[b][:], in_=rows[("y", b)][:, :FEATURES], func=ACT.Square,
                scale=math.sqrt(0.5), accum_out=half_sq[b][:, 0:1],
            )

        def square_products(b):
            if not in_batch(b):
                return
            features = grouped[("y", b)][:].rearrange("p (j c) -> p c j", c=PACK)
            bank = psum_products.tile([P, QUERY_TILES, P], F32, name="square", tag="products")
            for t in range(QUERY_TILES):
                for c in range(PACK):
                    block = features[:, c, (t + 1) * P : (t + 2) * P]
                    nc.tensor.matmul(bank[:, t, :], lhsT=block, rhs=block, start=c == 0, stop=c == PACK - 1)
            square[b] = bank

        def take_diagonals(b):
            if not in_batch(b):
                return
            for t in range(QUERY_TILES):
                diagonal_unread = scratch.tile([P, P], F32, name="diagonal_unread")
                nc.vector.scalar_tensor_tensor(
                    out=diagonal_unread[:], in0=square[b][:, t, :], scalar=0.5, in1=ident_f32[:],
                    op0=ALU.mult, op1=ALU.mult, accum_out=half_sq[b][:, t + 1 : t + 2],
                )

        def spread_half_sq(b):
            if not in_batch(b):
                return
            half_sq_spread[b] = psum_products.tile([P, POSITIONS], F32, name="half_sq_spread", tag="products")
            for r in range(KEY_BLOCKS):
                nc.tensor.transpose(
                    half_sq_spread[b][:, r * P : (r + 1) * P],
                    half_sq[b][:, r : r + 1].to_broadcast([P, P]),
                    ident_f32[:],
                )

        def copy_half_sq_spread(b):
            if not in_batch(b):
                return
            half_sq_of_keys[b] = norms.tile([P, POSITIONS], F32, name="half_sq_of_keys")
            nc.scalar.copy(out=half_sq_of_keys[b][:], in_=half_sq_spread[b][:])

        def transpose_rows(name, b):
            if not in_batch(b):
                return
            pairs = rows[(name, b)][:].bitcast(F32)
            transposed[(name, b)] = []
            for r0 in range(0, row_tiles[name], TILES_IN_BANK):
                count = min(TILES_IN_BANK, row_tiles[name] - r0)
                bank = psum_transposed.tile([P, count, PLANES, P], F32, name="rows_transposed", tag="transposed")
                for r in range(count):
                    for u in range(PLANES):
                        first = (r0 + r) * PAIRS + u * P
                        nc.tensor.transpose(bank[:, r, u, :], pairs[:, first : first + P], ident_f32[:])
                transposed[(name, b)].append((r0, count, bank))

        def copy_transposed_rows(name, b, copy):
            if not in_batch(b):
                return
            grouped[(name, b)] = group.tile([P, mx_columns[name] * PACK], BF16, name=name + "_grouped", align_bytes=64)
            pairs = grouped[(name, b)][:].bitcast(F32).rearrange("p (j u) -> p j u", u=PLANES)
            for r0, count, bank in transposed[(name, b)]:
                copy(
                    out=pairs[:, r0 * P : (r0 + count) * P, :].rearrange("p (r j) u -> p r j u", r=count),
                    in_=bank[:].rearrange("p r u j -> p r j u"),
                )

        def regroup_values(b, part):
            if not in_batch(b):
                return
            f0, size = VALUE_PARTS[part]
            tile = value_group.tile([P, size * PACK], BF16, name="v_grouped%d" % part, align_bytes=64)
            grouped[("v", b, part)] = tile
            nc.gpsimd.tensor_scalar(
                out=tile[:].rearrange("p (f c) -> p f c", c=PACK),
                in0=rows[("v", b)][:].rearrange("p (c f) -> p f c", c=PACK)[:, f0 : f0 + size, :],
                scalar1=1.0, scalar2=0.0, op0=ALU.mult, op1=ALU.add,
            )

        def quantise_values(b, part):
            if not in_batch(b):
                return
            if part == 0:
                words = value_packed.tile([P, FEATURES], U32, name="v_words", align_bytes=64)
                scales = value_packed.tile([P, FEATURES], U8, name="v_scales", align_bytes=64)
                codes[("v", b)] = (words, scales)
            words, scales = codes[("v", b)]
            f0, size = VALUE_PARTS[part]
            nc.vector.quantize_mx(
                out=words[:, f0 : f0 + size].bitcast(FP8X4), scales=scales[:, f0 : f0 + size],
                in_=grouped[("v", b, part)][:],
            )

        def quantise(name, b):
            if not in_batch(b):
                return
            words = packed.tile([P, mx_columns[name]], U32, name=name + "_words", align_bytes=64)
            scales = packed.tile([P, mx_columns[name]], U8, name=name + "_scales", align_bytes=64)
            for c0, size in power_pieces(mx_columns[name]):
                nc.vector.quantize_mx(
                    out=words[:, c0 : c0 + size].bitcast(FP8X4),
                    scales=scales[:, c0 : c0 + size],
                    in_=grouped[(name, b)][:, c0 * PACK : (c0 + size) * PACK],
                )
            codes[(name, b)] = (words, scales)


        def products(b, t):
            if not in_batch(b):
                return
            state[(b, t)] = {}
            for kind, left, right, c0 in (("scores", "q", "k", t * P), ("gram", "y", "y", (t + 1) * P)):
                bank = psum_products.tile([P, POSITIONS], F32, name=kind, tag="products")
                for k0, size in power_pieces(width_of(t)):
                    nc.tensor.matmul_mx(
                        out=bank[:, k0 : k0 + size],
                        lhsT=codes[(left, b)][0][:, c0 : c0 + P].bitcast(FP8X4),
                        lhsT_scale=codes[(left, b)][1][:, c0 : c0 + P],
                        rhs=codes[(right, b)][0][:, k0 : k0 + size].bitcast(FP8X4),
                        rhs_scale=codes[(right, b)][1][:, k0 : k0 + size],
                        start=True, stop=True,
                    )
                state[(b, t)][kind] = bank

        def lang_diagonal(b, t):
            if not in_batch(b):
                return
            tiles, width = state[(b, t)], width_of(t)
            tiles["lang"] = work.tile([P, POSITIONS], F32, name="lang")
            nc.vector.scalar_tensor_tensor(
                out=tiles["lang"][:, width - P : width], in0=tiles["scores"][:, width - P : width],
                scalar=-SCORE_SCALE, in1=mask[:], op0=ALU.mult, op1=ALU.subtract,
            )

        def lang_diagonal_minimum(b, t):
            if not in_batch(b):
                return
            tiles, width = state[(b, t)], width_of(t)
            tiles["diagonal_minimum"] = work.tile([P, 1], F32, name="diagonal_minimum")
            nc.vector.tensor_reduce(
                out=tiles["diagonal_minimum"][:], in_=tiles["lang"][:, width - P : width], axis=AXIS.X, op=ALU.min
            )

        def lang_before_diagonal(b, t):
            if not in_batch(b):
                return
            tiles, width = state[(b, t)], width_of(t)
            tiles["shift"] = work.tile([P, 1], F32, name="shift")
            nc.vector.tensor_scalar(
                out=tiles["lang"][:, : width - P], in0=tiles["scores"][:, : width - P], scalar1=-SCORE_SCALE,
                scalar2=tiles["diagonal_minimum"][:, 0:1], op0=ALU.mult, op1=ALU.min, accum_out=tiles["shift"][:, 0:1],
            )

        def row_minimum(b, t):
            if not in_batch(b):
                return
            tiles = state[(b, t)]
            tiles["shift"] = work.tile([P, 1], F32, name="shift")
            nc.gpsimd.tensor_scalar(
                out=tiles["shift"][:], in0=tiles["before_minimum"][:], scalar1=tiles["diagonal_minimum"][:, 0:1],
                scalar2=None, op0=ALU.min,
            )

        def grav_minus_key_norms(b, t, halves):
            if not in_batch(b):
                return
            tiles, width = state[(b, t)], width_of(t)
            if "grav" not in tiles:
                tiles["grav"] = work.tile([P, POSITIONS], F32, name="grav")
            for cols in (slice(0, width // 2), slice(width // 2, width))[halves]:
                nc.vector.tensor_tensor(
                    out=tiles["grav"][:, cols], in0=tiles["gram"][:, cols], in1=half_sq_of_keys[b][:, cols],
                    op=ALU.subtract,
                )

        def grav_before_diagonal(b, t):
            if not in_batch(b):
                return
            part = state[(b, t)]["grav"][:, : width_of(t) - P]
            nc.vector.tensor_scalar(
                out=part, in0=part, scalar1=half_sq[b][:, t + 1 : t + 2], scalar2=0.0, op0=ALU.subtract, op1=ALU.min,
            )

        def grav_diagonal(b, t):
            if not in_batch(b):
                return
            part = state[(b, t)]["grav"][:, width_of(t) - P : width_of(t)]
            nc.vector.scalar_tensor_tensor(
                out=part, in0=part, scalar=half_sq[b][:, t + 1 : t + 2], in1=mask[:], op0=ALU.subtract, op1=ALU.min,
            )

        def exponentials(b, t):
            if not in_batch(b):
                return
            tiles, width = state[(b, t)], width_of(t)
            tiles["sums"] = work.tile([P, 2, BLOCK_F32], F32, name="sums")
            nc.scalar.activation(
                out=tiles["lang"][:, :width], in_=tiles["lang"][:, :width], func=ACT.Exp,
                scale=-1.0, bias=tiles["shift"][:, 0:1], accum_out=tiles["sums"][:, 0, 0:1],
            )
            nc.scalar.activation(
                out=tiles["grav"][:, :width], in_=tiles["grav"][:, :width], func=ACT.Exp,
                scale=2.0 / (2.0 * FEATURES), accum_out=tiles["sums"][:, 1, 0:1],
            )

        def grav_denominator(b, t):
            if not in_batch(b):
                return
            kern_sum = state[(b, t)]["sums"][:, 1, 0:1]
            nc.vector.tensor_scalar(
                out=kern_sum, in0=kern_sum, scalar1=EPS, scalar2=1.0 / W_GRAV, op0=ALU.add, op1=ALU.mult,
            )

        def inverses(b, t):
            if not in_batch(b):
                return
            tiles = state[(b, t)]
            tiles["inverse"] = work.tile([P, 2], F32, name="inverse")
            nc.vector.reciprocal(out=tiles["inverse"][:], in_=tiles["sums"][:, :, 0])

        def lang_weights(b, t):
            if not in_batch(b):
                return
            tiles, width = state[(b, t)], width_of(t)
            nc.vector.tensor_scalar(
                out=tiles["lang"][:, :width], in0=tiles["lang"][:, :width], scalar1=tiles["inverse"][:, 0:1],
                scalar2=W_LANG, op0=ALU.mult, op1=ALU.mult,
            )

        def grav_weights(b, t):
            if not in_batch(b):
                return
            tiles, width = state[(b, t)], width_of(t)
            nc.vector.tensor_scalar(
                out=tiles["grav"][:, :width], in0=tiles["grav"][:, :width], scalar1=tiles["inverse"][:, 1:2],
                scalar2=None, op0=ALU.mult,
            )

        def transpose_weights(b, t):
            if not in_batch(b):
                return
            tiles = state[(b, t)]
            bank = psum_transposed.tile([P, t + 2, P], F32, name="weights_transposed", tag="transposed")
            for c in range(t + 2):
                cols = slice(c * P, (c + 1) * P)
                nc.tensor.matmul(
                    bank[:, c, :], lhsT=tiles["lang"][:, cols], rhs=ident_f32[:], is_transpose=True, start=True, stop=False
                )
                nc.tensor.matmul(
                    bank[:, c, :], lhsT=tiles["grav"][:, cols], rhs=ident_f32[:], is_transpose=True, start=False, stop=True
                )
            tiles["weights_transposed"] = bank

        def copy_transposed_weights(b, t):
            if not in_batch(b):
                return
            nc.scalar.copy(
                out=weights_grouped[t][:].rearrange("p (i c) -> p i c", c=PACK)[:, :, : t + 2],
                in_=state[(b, t)]["weights_transposed"][:].rearrange("p c i -> p i c"),
            )

        def quantise_weights(b, t):
            if not in_batch(b):
                return
            words = work.tile([P, P], U32, name="weights_words", align_bytes=64)
            scales = work.tile([P, P], U8, name="weights_scales", align_bytes=64)
            nc.vector.quantize_mx(out=words[:].bitcast(FP8X4), scales=scales[:], in_=weights_grouped[t][:])
            state[(b, t)]["weights_codes"] = (words, scales)

        def value_product(b, t):
            if not in_batch(b):
                return
            tiles = state[(b, t)]
            tiles["result"] = psum_products.tile([P, FEATURES], F32, name="result", tag="products")
            nc.tensor.matmul_mx(
                out=tiles["result"][:],
                lhsT=tiles["weights_codes"][0][:].bitcast(FP8X4), lhsT_scale=tiles["weights_codes"][1][:],
                rhs=codes[("v", b)][0][:].bitcast(FP8X4), rhs_scale=codes[("v", b)][1][:],
                start=True, stop=True,
            )

        def store(b, t):
            if not in_batch(b):
                return
            result_rows = work.tile([P, FEATURES], F32, name="result_rows")
            nc.scalar.copy(out=result_rows[:], in_=state[(b, t)]["result"][:])
            nc.sync.dma_start(out=out[b, t * P : (t + 1) * P, :], in_=result_rows[:])

        def tile_of(n):
            b, r = divmod(n, QUERY_TILES)
            return b, (r if b < BATCH - 1 else QUERY_TILES - 1 - r)

        ctx.enter_context(tc.manual_schedule())

        for n in range(-LOADS_AHEAD * QUERY_TILES, BATCH * QUERY_TILES + ROUNDS_TO_DRAIN):
            b, t = divmod(n, QUERY_TILES)
            entered = {back: tile_of(n - back) for back in range(-1, ROUNDS_TO_DRAIN + 1)}

            store(*entered[5])
            exponentials(*entered[1])

            lang_diagonal(*entered[0])
            grav_minus_key_norms(*entered[0], slice(0, 1))
            grav_denominator(*entered[2])
            lang_diagonal_minimum(*entered[0])
            grav_minus_key_norms(*entered[0], slice(1, 2))
            inverses(*entered[2])
            lang_before_diagonal(*entered[0])
            if t == 0:
                take_diagonals(b + 1)

            if t == 0:
                copy_transposed_rows("q", b + 1, nc.scalar.copy)
            if t == 1:
                copy_transposed_rows("y", b + 2, nc.scalar.copy)
            if t == 2:
                copy_transposed_rows("k", b + 2, nc.scalar.copy)

            lang_weights(*entered[2])
            quantise_weights(*entered[4])
            grav_before_diagonal(*entered[0])

            products(*entered[-1])
            value_product(*entered[4])
            if t == 2:
                square_products(b + 2)
            transpose_rows(("y", "k", "q")[t], b + 2)

            if t == 0:
                quantise("k", b + 1)
            if t == 1:
                quantise("q", b + 1)
            if t == 2:
                quantise("y", b + 2)
            grav_weights(*entered[2])
            grav_diagonal(*entered[0])
            quantise_values(b, t)
            regroup_values(b + 1, t)
            transpose_weights(*entered[2])

            copy_transposed_weights(*entered[3])
            if t == 1:
                copy_half_sq_spread(b + 1)
            if t == 0:
                sum_squares(b + 2)
            if t == 0:
                spread_half_sq(b + 1)
                load(b + LOADS_AHEAD)
